import numpy as np
import ml_dtypes


def mxq(x, axis, fmt="e4m3"):
    dtype, down = {"e4m3": (ml_dtypes.float8_e4m3fn, 7), "e5m2": (ml_dtypes.float8_e5m2, 14)}[fmt]
    v = np.moveaxis(np.asarray(x, np.float32).astype(ml_dtypes.bfloat16).astype(np.float64), axis, -1)
    blocks = v.reshape(v.shape[:-1] + (-1, 32))
    amax = np.abs(blocks).max(-1, keepdims=True)
    byte = np.maximum(np.where(amax > 0, np.frexp(amax)[1] - 1 + 127, 0) - down, 1)
    scale = np.exp2(byte - 127.0)
    codes = (blocks / scale).astype(np.float32).astype(dtype).astype(np.float64)
    return np.moveaxis((codes * scale).reshape(v.shape), -1, axis)


WIDE = False


def mx_kscale(k):
    if not WIDE:
        return np.ones(k)
    levels = np.array([10, -10, 5, -5, 0])
    a = np.random.permutation(np.resize(levels, k // 512 * 4)).reshape(k // 512, 4)
    idx = np.arange(k)
    return np.exp2(a[idx // 512, idx % 128 // 32])


BF16 = ml_dtypes.bfloat16


def bf(x):
    return np.asarray(x, np.float32).astype(BF16)


def f64(x):
    return np.asarray(x).astype(np.float64)


E2M1 = np.array([0.0, 0.5, 1.0, 1.5, 2.0, 3.0, 4.0, 6.0, -0.0, -0.5, -1.0, -1.5, -2.0, -3.0, -4.0, -6.0])


def pack_weight(w, fmt):
    k, n = w.shape
    w = f64(bf(w)).reshape(k // 32, 32, n)
    amax = np.abs(w).max(1)
    if fmt == "e4m3":
        byte = np.frexp(amax)[1] - 1 + 127 - 7
    else:
        mant, ex = np.frexp(amax / 6.0)
        byte = np.where(mant > 0.5, ex, ex - 1) + 127
    byte = np.clip(np.where(amax > 0, byte, 1), 1, 254)
    scaled = (w * np.exp2(127.0 - byte)[:, None, :]).reshape(k, n).astype(np.float32)
    by_word = np.ascontiguousarray(scaled.reshape(k // 512, 128, 4, n).transpose(0, 1, 3, 2))
    if fmt == "e4m3":
        words = by_word.astype(ml_dtypes.float8_e4m3fn).view(np.uint8)
    else:
        c = by_word.astype(ml_dtypes.float4_e2m1fn).view(np.uint8) & 0xF
        words = c[..., 0::2] | (c[..., 1::2] << 4)
    return np.ascontiguousarray(words), np.ascontiguousarray(byte.astype(np.uint8).reshape(k // 512, 16, n))


def unpack_weight(words, scales, fmt):
    g, p, n, _ = words.shape
    if fmt == "e4m3":
        vals = np.ascontiguousarray(words).view(ml_dtypes.float8_e4m3fn).astype(np.float64)
    else:
        nib = np.empty((g, p, n, 4), np.uint8)
        nib[..., 0::2] = words & 0xF
        nib[..., 1::2] = words >> 4
        vals = E2M1[nib]
    vals = vals * np.repeat(np.exp2(scales.astype(np.float64) - 127.0), 8, axis=1)[..., None]
    return vals.transpose(0, 1, 3, 2).reshape(g * 512, n)


B, D, O1, O2, O3 = 256, 1536, 8192, 512, 128
EPS = 1e-5
FMT = "e4m3"


def mish(v):
    return v * np.tanh(np.log(1.0 + np.exp(v)))


def sigmoid(v):
    return 1.0 / (1.0 + np.exp(-v))


def ln(u, g, b):
    mu = u.mean(-1, keepdims=True)
    var = np.square(u - mu).mean(-1, keepdims=True)
    return (u - mu) * (1.0 / np.sqrt(var + EPS)) * g + b


def setup_inputs():
    s = mx_kscale(O2)
    h_dec1 = bf(mish(np.random.standard_normal((B, O2))) * s)
    d2 = np.random.standard_normal((O1, O2)) * 1.5 / np.sqrt(O2) / s
    D2_words, D2_scales = pack_weight(np.ascontiguousarray(d2.T), FMT)
    g4 = bf(1.0 + 0.1 * np.random.standard_normal(O1))
    b4 = bf(0.1 * np.random.standard_normal(O1))
    d3 = np.random.standard_normal((D, O1)) * 1.5 / np.sqrt(O1)
    D3_words, D3_scales = pack_weight(np.ascontiguousarray(d3.T), FMT)
    bo = bf(0.3 * np.random.standard_normal(D))
    return {"h_dec1": h_dec1,
            "D2_words": D2_words,
            "D2_scales": D2_scales,
            "g4": g4,
            "b4": b4,
            "D3_words": D3_words,
            "D3_scales": D3_scales,
            "bo": bo}


def reference(h_dec1, D2_words, D2_scales, g4, b4, D3_words, D3_scales, bo):
    u = mxq(f64(h_dec1), 1, "e4m3") @ unpack_weight(D2_words, D2_scales, FMT)
    h = mish(ln(u, f64(g4), f64(b4)))
    return sigmoid((mxq(h, 1, "e4m3") @ unpack_weight(D3_words, D3_scales, FMT)) + f64(bo))

@@ -1,0 +1,276 @@
+from contextlib import ExitStack
+
+import concourse.mybir as mybir
+from concourse.masks import make_identity
+
+F32 = mybir.dt.float32
+BF16 = mybir.dt.bfloat16
+I32 = mybir.dt.int32
+U32 = mybir.dt.uint32
+U8 = mybir.dt.uint8
+FP8X4 = mybir.dt.float8_e4m3fn_x4
+ACT = mybir.ActivationFunctionType
+ALU = mybir.AluOpType
+
+P = 128
+PACK = 4
+K_PASS = P * PACK
+BATCH = 256
+BT = BATCH // P
+FEATS = 8192
+GROUPS = FEATS // K_PASS
+N_OUT = 1536
+N_TILE = 512
+NT = N_OUT // N_TILE
+EPS = 1e-5
+LN_FLOOR = 2.0 ** -60
+
+PLANES = 4
+D2_PLANE_COLS = FEATS // PLANES
+D2_CHUNK = 2 * K_PASS
+D2_BUFS = 4
+D3_BUFS = 10
+CHUNKS = 2
+CHUNK_GROUPS = GROUPS // CHUNKS
+ACT_BUFS = GROUPS + CHUNK_GROUPS + 2
+
+FLOPS = 2 * BATCH * K_PASS * FEATS + 2 * BATCH * FEATS * N_OUT
+
+
+def tile_autoencoder_pb_k_kernel(
+    tc, h_dec1, D2_words, D2_scales, g4, b4, D3_words, D3_scales, bo, out
+):
+    nc = tc.nc
+    with ExitStack() as ctx:
+        ctx.enter_context(tc.manual_schedule())
+        const = ctx.enter_context(tc.tile_pool(name="const", bufs=1))
+        d2_pool = ctx.enter_context(tc.tile_pool(name="d2", bufs=D2_BUFS))
+        d3_pool = ctx.enter_context(tc.tile_pool(name="d3", bufs=D3_BUFS))
+        act_pool = ctx.enter_context(tc.tile_pool(name="act", bufs=ACT_BUFS))
+        h_pool = ctx.enter_context(tc.tile_pool(name="h", bufs=3))
+        out_pool = ctx.enter_context(tc.tile_pool(name="outs", bufs=3))
+        psum_big = ctx.enter_context(tc.psum_pool(name="psum_big", bufs=BT * NT))
+        psum_tp = ctx.enter_context(tc.psum_pool(name="psum_tp", bufs=2))
+
+        x_sb = const.tile([P, BT, K_PASS], BF16)
+        nc.sync.dma_start(out=x_sb[:], in_=h_dec1.rearrange("(bt b) k -> b bt k", bt=BT))
+
+        ln_floor = const.tile([P, 1], F32)
+        nc.vector.memset(ln_floor[:], LN_FLOOR)
+        neg_half = const.tile([P, BT], F32)
+        nc.vector.memset(neg_half[:], -0.5)
+
+        d2_scales_sb = const.tile([P, D2_PLANE_COLS], U8, align_bytes=64)
+        nc.vector.memset(d2_scales_sb[:].bitcast(I32), 0)
+        d3_scales_sb = const.tile([P, GROUPS // PLANES, N_OUT], U8, align_bytes=64)
+        nc.vector.memset(d3_scales_sb[:].rearrange("p a n -> p (a n)").bitcast(I32), 0)
+        for quad in range(4):
+            nc.sync.dma_start(
+                out=d2_scales_sb[32 * quad : 32 * quad + 4 * PLANES, :].bitcast(I32),
+                in_=D2_scales[0, 4 * quad : 4 * quad + 4, :]
+                .rearrange("r (k n) -> k r n", k=PLANES)
+                .bitcast(I32),
+            )
+
+        gb_rows = const.tile([P, K_PASS], BF16)
+        nc.vector.memset(gb_rows[:], 0.0)
+        nc.scalar.dma_start(out=gb_rows[0:GROUPS, :], in_=g4.rearrange("(g k) -> g k", k=K_PASS))
+        nc.scalar.dma_start(
+            out=gb_rows[GROUPS : 2 * GROUPS, :], in_=b4.rearrange("(g k) -> g k", k=K_PASS)
+        )
+        bo_bc = const.tile([P, N_OUT], BF16)
+        nc.scalar.dma_start(out=bo_bc[:], in_=bo.partition_broadcast(P))
+
+        warm = const.tile([P, 1], F32)
+
+        def load_sigmoid_table():
+            nc.scalar.activation(out=warm[:], in_=ln_floor[:], func=ACT.Sigmoid)
+
+        load_sigmoid_table()
+
+        ident = const.tile([P, P], F32)
+        make_identity(nc, ident[:])
+
+        xT_ps = psum_tp.tile([P, BT, 2, P], F32, tag="tp")
+        for bt in range(BT):
+            x_words = x_sb[:, bt, :].bitcast(F32)
+            for u in range(2):
+                nc.tensor.transpose(xT_ps[:, bt, u, :], x_words[:, u : K_PASS // 2 : 2], ident[:])
+        x_grouped = const.tile([P, BATCH * PACK], BF16, align_bytes=64)
+        nc.vector.tensor_copy(
+            out=x_grouped[:].bitcast(F32).rearrange("p (bt b u) -> p bt b u", bt=BT, u=2),
+            in_=xT_ps[:].rearrange("p bt u b -> p bt b u"),
+        )
+        x_codes = const.tile([P, BATCH], U32, align_bytes=64)
+        x_scales = const.tile([P, BATCH], U8, align_bytes=64)
+        nc.vector.quantize_mx(out=x_codes[:].bitcast(FP8X4), scales=x_scales[:], in_=x_grouped[:])
+
+        gb_sorted = const.tile([P, PACK, P], F32)
+        nc.vector.tensor_copy(out=gb_sorted[:], in_=gb_rows[:].rearrange("r (p t) -> r t p", t=PACK))
+        gbT_ps = psum_tp.tile([P, PACK, P], F32, tag="tp")
+        for t in range(PACK):
+            nc.tensor.transpose(gbT_ps[:, t, :], gb_sorted[:, t, :], ident[:])
+        gb_cols = const.tile([P, PACK, 2 * GROUPS], F32)
+        nc.vector.tensor_copy(out=gb_cols[:], in_=gbT_ps[:, :, 0 : 2 * GROUPS])
+
+        d2_words_i32 = D2_words[0].rearrange("p n t -> p (n t)").bitcast(I32)
+        stats = const.tile([P, BT, GROUPS, 6], F32)
+        u_tiles = []
+        for c in range(FEATS // D2_CHUNK):
+            d2w = d2_pool.tile([P, D2_CHUNK], I32, align_bytes=64)
+            nc.sync.dma_start(out=d2w[:], in_=d2_words_i32[:, c * D2_CHUNK : (c + 1) * D2_CHUNK])
+            for j in range(D2_CHUNK // K_PASS):
+                g = c * (D2_CHUNK // K_PASS) + j
+                plane, col = divmod(g * K_PASS, D2_PLANE_COLS)
+                u_sb = act_pool.tile([P, BT, PACK, P], F32, tag="act", name="u%d" % g)
+                u_tiles.append(u_sb)
+                for bt in range(BT):
+                    u_ps = psum_big.tile([P, K_PASS], F32, tag="big")
+                    nc.tensor.matmul_mx(
+                        out=u_ps[:],
+                        lhsT=x_codes[:, bt * P : (bt + 1) * P].bitcast(FP8X4),
+                        lhsT_scale=x_scales[:, bt * P : (bt + 1) * P],
+                        rhs=d2w[:, j * K_PASS : (j + 1) * K_PASS].bitcast(FP8X4),
+                        rhs_scale=d2_scales_sb[4 * plane : P, col : col + K_PASS],
+                        start=True,
+                        stop=True,
+                    )
+                    nc.scalar.copy(
+                        out=u_sb[:, bt, :, :], in_=u_ps[:].rearrange("b (p t) -> b t p", t=PACK)
+                    )
+                    nc.vector.bn_stats(out=stats[:, bt, g, :], in_=u_sb[:, bt, :, :])
+
+        for a in range(GROUPS // PLANES):
+            for quad in range(4):
+                nc.sync.dma_start(
+                    out=d3_scales_sb[32 * quad : 32 * quad + 4 * PLANES, a, :].bitcast(I32),
+                    in_=D3_scales[PLANES * a : PLANES * (a + 1), 4 * quad : 4 * quad + 4, :].bitcast(I32),
+                )
+
+        d3_tiles = {}
+
+        def load_d3(chunk):
+            for g in range(chunk * CHUNK_GROUPS, (chunk + 1) * CHUNK_GROUPS):
+                d3w = d3_pool.tile([P, N_OUT], I32, align_bytes=64, tag="d3w", name="d3w%d" % g)
+                nc.sync.dma_start(
+                    out=d3w[:], in_=D3_words[g].rearrange("p n t -> p (n t)").bitcast(I32)
+                )
+                d3_tiles[g] = d3w
+
+        load_d3(0)
+
+        mean_var = const.tile([P, BT, 2], F32)
+        for bt in range(BT):
+            nc.vector.bn_aggr(out=mean_var[:, bt, :], in_=stats[:, bt, :, :].rearrange("p g s -> p (g s)"))
+        var_eps = const.tile([P, BT], F32)
+        nc.vector.tensor_scalar_add(out=var_eps[:], in0=mean_var[:, :, 1], scalar1=EPS)
+        rstd = const.tile([P, BT], F32)
+        nc.gpsimd.tensor_tensor(out=rstd[:], in0=var_eps[:], in1=neg_half[:], op=ALU.pow)
+
+        acc = [
+            [psum_big.tile([P, N_TILE], F32, tag="big", name="acc%d_%d" % (bt, nt)) for nt in range(NT)]
+            for bt in range(BT)
+        ]
+        v_tiles = {}
+        e_tiles = {}
+
+        def normalise(g):
+            for bt in range(BT):
+                nc.vector.tensor_scalar(
+                    out=u_tiles[g][:, bt, :, :],
+                    in0=u_tiles[g][:, bt, :, :],
+                    scalar1=mean_var[:, bt, 0:1],
+                    scalar2=rstd[:, bt : bt + 1],
+                    op0=ALU.subtract,
+                    op1=ALU.mult,
+                )
+
+        def transpose_and_scale(g):
+            v_sb = act_pool.tile([P, PACK, BATCH], F32, tag="act", name="v%d" % g)
+            v_tiles[g] = v_sb
+            for half in range(2):
+                zT_ps = psum_tp.tile([P, 2, BATCH], F32, tag="tp")
+                for i in range(2):
+                    for bt in range(BT):
+                        nc.tensor.transpose(
+                            zT_ps[:, i, bt * P : (bt + 1) * P], u_tiles[g][:, bt, 2 * half + i, :], ident[:]
+                        )
+                for i in range(2):
+                    t = 2 * half + i
+                    nc.vector.tensor_scalar(
+                        out=v_sb[:, t, :],
+                        in0=zT_ps[:, i, :],
+                        scalar1=gb_cols[:, t, g : g + 1],
+                        scalar2=gb_cols[:, t, GROUPS + g : GROUPS + g + 1],
+                        op0=ALU.mult,
+                        op1=ALU.add,
+                    )
+
+        def prepare(chunk):
+            first = chunk * CHUNK_GROUPS
+            last = first + CHUNK_GROUPS - 1
+            normalise(first)
+            for g in range(first, last + 1):
+                if g < last:
+                    normalise(g + 1)
+                transpose_and_scale(g)
+
+        def sigmoids(chunk):
+            for g in range(chunk * CHUNK_GROUPS, (chunk + 1) * CHUNK_GROUPS):
+                e_sb = act_pool.tile([P, PACK, BATCH], F32, tag="act", name="e%d" % g)
+                e_tiles[g] = e_sb
+                nc.scalar.activation(out=e_sb[:], in_=v_tiles[g][:], func=ACT.Sigmoid, scale=-1.0)
+
+        def logs(chunk):
+            for g in range(chunk * CHUNK_GROUPS, (chunk + 1) * CHUNK_GROUPS):
+                nc.scalar.activation(out=e_tiles[g][:], in_=e_tiles[g][:], func=ACT.Ln, bias=ln_floor[:])
+
+        def finish(chunk):
+            load_sigmoid_table()
+            for g in range(chunk * CHUNK_GROUPS, (chunk + 1) * CHUNK_GROUPS):
+                nc.scalar.activation(out=e_tiles[g][:], in_=e_tiles[g][:], func=ACT.Tanh, scale=-1.0)
+                h_grouped = h_pool.tile([P, BATCH, PACK], BF16, align_bytes=64)
+                nc.vector.tensor_tensor(
+                    out=h_grouped[:],
+                    in0=v_tiles[g][:].rearrange("p t b -> p b t"),
+                    in1=e_tiles[g][:].rearrange("p t b -> p b t"),
+                    op=ALU.mult,
+                )
+                h_codes = h_pool.tile([P, BATCH], U32, align_bytes=64)
+                h_scales = h_pool.tile([P, BATCH], U8, align_bytes=64)
+                nc.vector.quantize_mx(
+                    out=h_codes[:].bitcast(FP8X4),
+                    scales=h_scales[:],
+                    in_=h_grouped[:].rearrange("p b t -> p (b t)"),
+                )
+                a, k = divmod(g, PLANES)
+                for bt in range(BT):
+                    for nt in range(NT):
+                        nc.tensor.matmul_mx(
+                            out=acc[bt][nt][:],
+                            lhsT=h_codes[:, bt * P : (bt + 1) * P].bitcast(FP8X4),
+                            lhsT_scale=h_scales[:, bt * P : (bt + 1) * P],
+                            rhs=d3_tiles[g][:, nt * N_TILE : (nt + 1) * N_TILE].bitcast(FP8X4),
+                            rhs_scale=d3_scales_sb[4 * k : P, a, nt * N_TILE : (nt + 1) * N_TILE],
+                            start=(g == 0),
+                            stop=(g == GROUPS - 1),
+                        )
+
+        prepare(0)
+        sigmoids(0)
+        for chunk in range(CHUNKS):
+            if chunk + 1 < CHUNKS:
+                prepare(chunk + 1)
+            logs(chunk)
+            finish(chunk)
+            if chunk + 1 < CHUNKS:
+                load_d3(chunk + 1)
+                sigmoids(chunk + 1)
+
+        for bt in range(BT):
+            for nt in range(NT):
+                cols = slice(nt * N_TILE, (nt + 1) * N_TILE)
+                y_sb = out_pool.tile([P, N_TILE], F32)
+                nc.vector.tensor_tensor(out=y_sb[:], in0=acc[bt][nt][:], in1=bo_bc[:, cols], op=ALU.add)
+                nc.scalar.activation(out=y_sb[:], in_=y_sb[:], func=ACT.Sigmoid)
+                nc.sync.dma_start(out=out[bt * P : (bt + 1) * P, cols], in_=y_sb[:])

@@ -28,8 +28,7 @@ LN_FLOOR = 2.0 ** -60
 PLANES = 4
 D2_PLANE_COLS = FEATS // PLANES
 D2_CHUNK = 2 * K_PASS
-D2_BUFS = 4
-D3_BUFS = 10
+D3_BUFS = 8
 CHUNKS = 2
 CHUNK_GROUPS = GROUPS // CHUNKS
 ACT_BUFS = GROUPS + CHUNK_GROUPS + 2
@@ -44,7 +43,6 @@ def tile_autoencoder_pb_k_kernel(
     with ExitStack() as ctx:
         ctx.enter_context(tc.manual_schedule())
         const = ctx.enter_context(tc.tile_pool(name="const", bufs=1))
-        d2_pool = ctx.enter_context(tc.tile_pool(name="d2", bufs=D2_BUFS))
         d3_pool = ctx.enter_context(tc.tile_pool(name="d3", bufs=D3_BUFS))
         act_pool = ctx.enter_context(tc.tile_pool(name="act", bufs=ACT_BUFS))
         h_pool = ctx.enter_context(tc.tile_pool(name="h", bufs=3))
@@ -57,7 +55,7 @@ def tile_autoencoder_pb_k_kernel(
 
         ln_floor = const.tile([P, 1], F32)
         nc.vector.memset(ln_floor[:], LN_FLOOR)
-        neg_half = const.tile([P, BT], F32)
+        neg_half = const.tile([P, 1], F32)
         nc.vector.memset(neg_half[:], -0.5)
 
         d2_scales_sb = const.tile([P, D2_PLANE_COLS], U8, align_bytes=64)
@@ -114,31 +112,67 @@ def tile_autoencoder_pb_k_kernel(
         nc.vector.tensor_copy(out=gb_cols[:], in_=gbT_ps[:, :, 0 : 2 * GROUPS])
 
         d2_words_i32 = D2_words[0].rearrange("p n t -> p (n t)").bitcast(I32)
-        stats = const.tile([P, BT, GROUPS, 6], F32)
-        u_tiles = []
+        d2w = const.tile([P, FEATS], I32, align_bytes=64)
         for c in range(FEATS // D2_CHUNK):
-            d2w = d2_pool.tile([P, D2_CHUNK], I32, align_bytes=64)
-            nc.sync.dma_start(out=d2w[:], in_=d2_words_i32[:, c * D2_CHUNK : (c + 1) * D2_CHUNK])
-            for j in range(D2_CHUNK // K_PASS):
-                g = c * (D2_CHUNK // K_PASS) + j
+            cols = slice(c * D2_CHUNK, (c + 1) * D2_CHUNK)
+            nc.sync.dma_start(out=d2w[:, cols], in_=d2_words_i32[:, cols])
+
+        u_tiles = [
+            act_pool.tile([P, BT, PACK, P], F32, tag="act", name="u%d" % g) for g in range(GROUPS)
+        ]
+        stats = const.tile([P, BT, GROUPS, 6], F32)
+        mean_var = const.tile([P, BT, 2], F32)
+        neg_mean = const.tile([P, BT], F32)
+        var_eps = const.tile([P, BT], F32)
+        rstd = [const.tile([P, 1], F32, name="rstd%d" % bt) for bt in range(BT)]
+
+        def first_product(bt):
+            for g in range(GROUPS):
                 plane, col = divmod(g * K_PASS, D2_PLANE_COLS)
-                u_sb = act_pool.tile([P, BT, PACK, P], F32, tag="act", name="u%d" % g)
-                u_tiles.append(u_sb)
-                for bt in range(BT):
-                    u_ps = psum_big.tile([P, K_PASS], F32, tag="big")
-                    nc.tensor.matmul_mx(
-                        out=u_ps[:],
-                        lhsT=x_codes[:, bt * P : (bt + 1) * P].bitcast(FP8X4),
-                        lhsT_scale=x_scales[:, bt * P : (bt + 1) * P],
-                        rhs=d2w[:, j * K_PASS : (j + 1) * K_PASS].bitcast(FP8X4),
-                        rhs_scale=d2_scales_sb[4 * plane : P, col : col + K_PASS],
-                        start=True,
-                        stop=True,
-                    )
-                    nc.scalar.copy(
-                        out=u_sb[:, bt, :, :], in_=u_ps[:].rearrange("b (p t) -> b t p", t=PACK)
-                    )
-                    nc.vector.bn_stats(out=stats[:, bt, g, :], in_=u_sb[:, bt, :, :])
+                u_ps = psum_big.tile([P, K_PASS], F32, tag="big")
+                nc.tensor.matmul_mx(
+                    out=u_ps[:],
+                    lhsT=x_codes[:, bt * P : (bt + 1) * P].bitcast(FP8X4),
+                    lhsT_scale=x_scales[:, bt * P : (bt + 1) * P],
+                    rhs=d2w[:, g * K_PASS : (g + 1) * K_PASS].bitcast(FP8X4),
+                    rhs_scale=d2_scales_sb[4 * plane : P, col : col + K_PASS],
+                    start=True,
+                    stop=True,
+                )
+                nc.scalar.copy(
+                    out=u_tiles[g][:, bt, :, :], in_=u_ps[:].rearrange("b (p t) -> b t p", t=PACK)
+                )
+                nc.vector.bn_stats(out=stats[:, bt, g, :], in_=u_tiles[g][:, bt, :, :])
+
+        def statistics(bt):
+            nc.vector.bn_aggr(
+                out=mean_var[:, bt, :], in_=stats[:, bt, :, :].rearrange("p g s -> p (g s)")
+            )
+            nc.vector.tensor_scalar_add(
+                out=var_eps[:, bt : bt + 1], in0=mean_var[:, bt, 1:2], scalar1=EPS
+            )
+            nc.gpsimd.tensor_tensor(
+                out=rstd[bt][:], in0=var_eps[:, bt : bt + 1], in1=neg_half[:], op=ALU.pow
+            )
+            nc.vector.tensor_scalar_mul(
+                out=neg_mean[:, bt : bt + 1], in0=mean_var[:, bt, 0:1], scalar1=-1.0
+            )
+
+        def normalise(bt, chunk):
+            for g in range(chunk * CHUNK_GROUPS, (chunk + 1) * CHUNK_GROUPS):
+                nc.gpsimd.tensor_scalar(
+                    out=u_tiles[g][:, bt, :, :],
+                    in0=u_tiles[g][:, bt, :, :],
+                    scalar1=neg_mean[:, bt : bt + 1],
+                    scalar2=rstd[bt][:],
+                    op0=ALU.add,
+                    op1=ALU.mult,
+                )
+
+        for bt in range(BT):
+            first_product(bt)
+            statistics(bt)
+            normalise(bt, 0)
 
         for a in range(GROUPS // PLANES):
             for quad in range(4):
@@ -159,31 +193,12 @@ def tile_autoencoder_pb_k_kernel(
 
         load_d3(0)
 
-        mean_var = const.tile([P, BT, 2], F32)
-        for bt in range(BT):
-            nc.vector.bn_aggr(out=mean_var[:, bt, :], in_=stats[:, bt, :, :].rearrange("p g s -> p (g s)"))
-        var_eps = const.tile([P, BT], F32)
-        nc.vector.tensor_scalar_add(out=var_eps[:], in0=mean_var[:, :, 1], scalar1=EPS)
-        rstd = const.tile([P, BT], F32)
-        nc.gpsimd.tensor_tensor(out=rstd[:], in0=var_eps[:], in1=neg_half[:], op=ALU.pow)
-
         acc = [
             [psum_big.tile([P, N_TILE], F32, tag="big", name="acc%d_%d" % (bt, nt)) for nt in range(NT)]
             for bt in range(BT)
         ]
         v_tiles = {}
         e_tiles = {}
-
-        def normalise(g):
-            for bt in range(BT):
-                nc.vector.tensor_scalar(
-                    out=u_tiles[g][:, bt, :, :],
-                    in0=u_tiles[g][:, bt, :, :],
-                    scalar1=mean_var[:, bt, 0:1],
-                    scalar2=rstd[:, bt : bt + 1],
-                    op0=ALU.subtract,
-                    op1=ALU.mult,
-                )
 
         def transpose_and_scale(g):
             v_sb = act_pool.tile([P, PACK, BATCH], F32, tag="act", name="v%d" % g)
@@ -207,12 +222,7 @@ def tile_autoencoder_pb_k_kernel(
                     )
 
         def prepare(chunk):
-            first = chunk * CHUNK_GROUPS
-            last = first + CHUNK_GROUPS - 1
-            normalise(first)
-            for g in range(first, last + 1):
-                if g < last:
-                    normalise(g + 1)
+            for g in range(chunk * CHUNK_GROUPS, (chunk + 1) * CHUNK_GROUPS):
                 transpose_and_scale(g)
 
         def sigmoids(chunk):
@@ -225,41 +235,55 @@ def tile_autoencoder_pb_k_kernel(
             for g in range(chunk * CHUNK_GROUPS, (chunk + 1) * CHUNK_GROUPS):
                 nc.scalar.activation(out=e_tiles[g][:], in_=e_tiles[g][:], func=ACT.Ln, bias=ln_floor[:])
 
+        h_tiles = {}
+
+        def tanh_and_multiply(g):
+            nc.scalar.activation(out=e_tiles[g][:], in_=e_tiles[g][:], func=ACT.Tanh, scale=-1.0)
+            h_grouped = h_pool.tile([P, BATCH, PACK], BF16, align_bytes=64)
+            h_tiles[g] = h_grouped
+            nc.vector.tensor_tensor(
+                out=h_grouped[:].rearrange("p (c i) t -> p c t i", i=4),
+                in0=v_tiles[g][:].rearrange("p t (c i) -> p c t i", i=4),
+                in1=e_tiles[g][:].rearrange("p t (c i) -> p c t i", i=4),
+                op=ALU.mult,
+            )
+
+        def second_product(g):
+            h_codes = h_pool.tile([P, BATCH], U32, align_bytes=64)
+            h_scales = h_pool.tile([P, BATCH], U8, align_bytes=64)
+            nc.vector.quantize_mx(
+                out=h_codes[:].bitcast(FP8X4),
+                scales=h_scales[:],
+                in_=h_tiles[g][:].rearrange("p b t -> p (b t)"),
+            )
+            a, k = divmod(g, PLANES)
+            for bt in range(BT):
+                for nt in range(NT):
+                    nc.tensor.matmul_mx(
+                        out=acc[bt][nt][:],
+                        lhsT=h_codes[:, bt * P : (bt + 1) * P].bitcast(FP8X4),
+                        lhsT_scale=h_scales[:, bt * P : (bt + 1) * P],
+                        rhs=d3_tiles[g][:, nt * N_TILE : (nt + 1) * N_TILE].bitcast(FP8X4),
+                        rhs_scale=d3_scales_sb[4 * k : P, a, nt * N_TILE : (nt + 1) * N_TILE],
+                        start=(g == 0),
+                        stop=(g == GROUPS - 1),
+                    )
+
         def finish(chunk):
+            first = chunk * CHUNK_GROUPS
             load_sigmoid_table()
-            for g in range(chunk * CHUNK_GROUPS, (chunk + 1) * CHUNK_GROUPS):
-                nc.scalar.activation(out=e_tiles[g][:], in_=e_tiles[g][:], func=ACT.Tanh, scale=-1.0)
-                h_grouped = h_pool.tile([P, BATCH, PACK], BF16, align_bytes=64)
-                nc.vector.tensor_tensor(
-                    out=h_grouped[:],
-                    in0=v_tiles[g][:].rearrange("p t b -> p b t"),
-                    in1=e_tiles[g][:].rearrange("p t b -> p b t"),
-                    op=ALU.mult,
-                )
-                h_codes = h_pool.tile([P, BATCH], U32, align_bytes=64)
-                h_scales = h_pool.tile([P, BATCH], U8, align_bytes=64)
-                nc.vector.quantize_mx(
-                    out=h_codes[:].bitcast(FP8X4),
-                    scales=h_scales[:],
-                    in_=h_grouped[:].rearrange("p b t -> p (b t)"),
-                )
-                a, k = divmod(g, PLANES)
-                for bt in range(BT):
-                    for nt in range(NT):
-                        nc.tensor.matmul_mx(
-                            out=acc[bt][nt][:],
-                            lhsT=h_codes[:, bt * P : (bt + 1) * P].bitcast(FP8X4),
-                            lhsT_scale=h_scales[:, bt * P : (bt + 1) * P],
-                            rhs=d3_tiles[g][:, nt * N_TILE : (nt + 1) * N_TILE].bitcast(FP8X4),
-                            rhs_scale=d3_scales_sb[4 * k : P, a, nt * N_TILE : (nt + 1) * N_TILE],
-                            start=(g == 0),
-                            stop=(g == GROUPS - 1),
-                        )
+            for g in range(first, first + CHUNK_GROUPS):
+                tanh_and_multiply(g)
+                if g > first:
+                    second_product(g - 1)
+            second_product(first + CHUNK_GROUPS - 1)
 
         prepare(0)
         sigmoids(0)
         for chunk in range(CHUNKS):
             if chunk + 1 < CHUNKS:
+                for bt in range(BT):
+                    normalise(bt, chunk + 1)
                 prepare(chunk + 1)
             logs(chunk)
             finish(chunk)

@@ -27,11 +27,13 @@ LN_FLOOR = 2.0 ** -60
 
 PLANES = 4
 D2_PLANE_COLS = FEATS // PLANES
-D2_CHUNK = 2 * K_PASS
-D3_BUFS = 8
-CHUNKS = 2
-CHUNK_GROUPS = GROUPS // CHUNKS
-ACT_BUFS = GROUPS + CHUNK_GROUPS + 2
+D2_TILE_GROUPS = N_OUT // K_PASS
+D2_TILES = (GROUPS + D2_TILE_GROUPS - 1) // D2_TILE_GROUPS
+W_BUFS = GROUPS
+D3_EARLY = W_BUFS - D2_TILES
+PAIRS = GROUPS // 2
+E_BUFS = PAIRS + PAIRS // 2
+KEPT = GROUPS // 2
 
 FLOPS = 2 * BATCH * K_PASS * FEATS + 2 * BATCH * FEATS * N_OUT
 
@@ -43,14 +45,14 @@ def tile_autoencoder_pb_k_kernel(
     with ExitStack() as ctx:
         ctx.enter_context(tc.manual_schedule())
         const = ctx.enter_context(tc.tile_pool(name="const", bufs=1))
-        d3_pool = ctx.enter_context(tc.tile_pool(name="d3", bufs=D3_BUFS))
-        act_pool = ctx.enter_context(tc.tile_pool(name="act", bufs=ACT_BUFS))
+        w_pool = ctx.enter_context(tc.tile_pool(name="weights", bufs=W_BUFS))
+        u_pool = ctx.enter_context(tc.tile_pool(name="u", bufs=BT * PAIRS))
+        e_pool = ctx.enter_context(tc.tile_pool(name="e", bufs=E_BUFS))
         h_pool = ctx.enter_context(tc.tile_pool(name="h", bufs=3))
-        out_pool = ctx.enter_context(tc.tile_pool(name="outs", bufs=3))
-        psum_big = ctx.enter_context(tc.psum_pool(name="psum_big", bufs=BT * NT))
-        psum_tp = ctx.enter_context(tc.psum_pool(name="psum_tp", bufs=2))
+        psum_big = ctx.enter_context(tc.psum_pool(name="psum_big", bufs=4))
+        psum_tp = ctx.enter_context(tc.psum_pool(name="psum_tp", bufs=4))
 
-        x_sb = const.tile([P, BT, K_PASS], BF16)
+        x_sb = e_pool.tile([P, BT, K_PASS], BF16, align_bytes=64, tag="e")
         nc.sync.dma_start(out=x_sb[:], in_=h_dec1.rearrange("(bt b) k -> b bt k", bt=BT))
 
         ln_floor = const.tile([P, 1], F32)
@@ -60,8 +62,6 @@ def tile_autoencoder_pb_k_kernel(
 
         d2_scales_sb = const.tile([P, D2_PLANE_COLS], U8, align_bytes=64)
         nc.vector.memset(d2_scales_sb[:].bitcast(I32), 0)
-        d3_scales_sb = const.tile([P, GROUPS // PLANES, N_OUT], U8, align_bytes=64)
-        nc.vector.memset(d3_scales_sb[:].rearrange("p a n -> p (a n)").bitcast(I32), 0)
         for quad in range(4):
             nc.sync.dma_start(
                 out=d2_scales_sb[32 * quad : 32 * quad + 4 * PLANES, :].bitcast(I32),
@@ -70,21 +70,31 @@ def tile_autoencoder_pb_k_kernel(
                 .bitcast(I32),
             )
 
-        gb_rows = const.tile([P, K_PASS], BF16)
-        nc.vector.memset(gb_rows[:], 0.0)
-        nc.scalar.dma_start(out=gb_rows[0:GROUPS, :], in_=g4.rearrange("(g k) -> g k", k=K_PASS))
-        nc.scalar.dma_start(
-            out=gb_rows[GROUPS : 2 * GROUPS, :], in_=b4.rearrange("(g k) -> g k", k=K_PASS)
-        )
-        bo_bc = const.tile([P, N_OUT], BF16)
-        nc.scalar.dma_start(out=bo_bc[:], in_=bo.partition_broadcast(P))
-
         warm = const.tile([P, 1], F32)
 
         def load_sigmoid_table():
             nc.scalar.activation(out=warm[:], in_=ln_floor[:], func=ACT.Sigmoid)
 
         load_sigmoid_table()
+
+        gb_rows = e_pool.tile([P, K_PASS], BF16, align_bytes=64, tag="e")
+        nc.vector.memset(gb_rows[:], 0.0)
+        nc.scalar.dma_start(out=gb_rows[0:GROUPS, :], in_=g4.rearrange("(g k) -> g k", k=K_PASS))
+        nc.scalar.dma_start(
+            out=gb_rows[GROUPS : 2 * GROUPS, :], in_=b4.rearrange("(g k) -> g k", k=K_PASS)
+        )
+
+        d2_words_i32 = D2_words[0].rearrange("p n t -> p (n t)").bitcast(I32)
+        d2_tiles = []
+        for c in range(D2_TILES):
+            d2w = w_pool.tile([P, N_OUT], I32, align_bytes=64, tag="w", name="d2w%d" % c)
+            d2_tiles.append(d2w)
+            for i in range(min(D2_TILE_GROUPS, GROUPS - c * D2_TILE_GROUPS)):
+                g = c * D2_TILE_GROUPS + i
+                nc.sync.dma_start(
+                    out=d2w[:, i * K_PASS : (i + 1) * K_PASS],
+                    in_=d2_words_i32[:, g * K_PASS : (g + 1) * K_PASS],
+                )
 
         ident = const.tile([P, P], F32)
         make_identity(nc, ident[:])
@@ -94,7 +104,7 @@ def tile_autoencoder_pb_k_kernel(
             x_words = x_sb[:, bt, :].bitcast(F32)
             for u in range(2):
                 nc.tensor.transpose(xT_ps[:, bt, u, :], x_words[:, u : K_PASS // 2 : 2], ident[:])
-        x_grouped = const.tile([P, BATCH * PACK], BF16, align_bytes=64)
+        x_grouped = e_pool.tile([P, BATCH * PACK], BF16, align_bytes=64, tag="e")
         nc.vector.tensor_copy(
             out=x_grouped[:].bitcast(F32).rearrange("p (bt b u) -> p bt b u", bt=BT, u=2),
             in_=xT_ps[:].rearrange("p bt u b -> p bt b u"),
@@ -103,22 +113,35 @@ def tile_autoencoder_pb_k_kernel(
         x_scales = const.tile([P, BATCH], U8, align_bytes=64)
         nc.vector.quantize_mx(out=x_codes[:].bitcast(FP8X4), scales=x_scales[:], in_=x_grouped[:])
 
-        gb_sorted = const.tile([P, PACK, P], F32)
-        nc.vector.tensor_copy(out=gb_sorted[:], in_=gb_rows[:].rearrange("r (p t) -> r t p", t=PACK))
-        gbT_ps = psum_tp.tile([P, PACK, P], F32, tag="tp")
-        for t in range(PACK):
-            nc.tensor.transpose(gbT_ps[:, t, :], gb_sorted[:, t, :], ident[:])
-        gb_cols = const.tile([P, PACK, 2 * GROUPS], F32)
-        nc.vector.tensor_copy(out=gb_cols[:], in_=gbT_ps[:, :, 0 : 2 * GROUPS])
+        d3_scales_sb = const.tile([P, GROUPS // PLANES, N_OUT], U8, align_bytes=64)
+        nc.vector.memset(d3_scales_sb[:].rearrange("p a n -> p (a n)").bitcast(I32), 0)
+        for a in range(GROUPS // PLANES):
+            for quad in range(4):
+                nc.sync.dma_start(
+                    out=d3_scales_sb[32 * quad : 32 * quad + 4 * PLANES, a, :].bitcast(I32),
+                    in_=D3_scales[PLANES * a : PLANES * (a + 1), 4 * quad : 4 * quad + 4, :].bitcast(I32),
+                )
 
-        d2_words_i32 = D2_words[0].rearrange("p n t -> p (n t)").bitcast(I32)
-        d2w = const.tile([P, FEATS], I32, align_bytes=64)
-        for c in range(FEATS // D2_CHUNK):
-            cols = slice(c * D2_CHUNK, (c + 1) * D2_CHUNK)
-            nc.sync.dma_start(out=d2w[:, cols], in_=d2_words_i32[:, cols])
+        d3_tiles = []
+
+        def load_d3(first, last):
+            for g in range(first, last):
+                d3w = w_pool.tile([P, N_OUT], I32, align_bytes=64, tag="w", name="d3w%d" % g)
+                nc.sync.dma_start(
+                    out=d3w[:], in_=D3_words[g].rearrange("p n t -> p (n t)").bitcast(I32)
+                )
+                d3_tiles.append(d3w)
+
+        load_d3(0, D3_EARLY)
 
         u_tiles = [
-            act_pool.tile([P, BT, PACK, P], F32, tag="act", name="u%d" % g) for g in range(GROUPS)
+            [
+                u_pool.tile(
+                    [P, 2, PACK, P], F32, align_bytes=64, tag="u", name="u%d_%d" % (bt, pair)
+                )
+                for pair in range(PAIRS)
+            ]
+            for bt in range(BT)
         ]
         stats = const.tile([P, BT, GROUPS, 6], F32)
         mean_var = const.tile([P, BT, 2], F32)
@@ -126,23 +149,33 @@ def tile_autoencoder_pb_k_kernel(
         var_eps = const.tile([P, BT], F32)
         rstd = [const.tile([P, 1], F32, name="rstd%d" % bt) for bt in range(BT)]
 
-        def first_product(bt):
-            for g in range(GROUPS):
-                plane, col = divmod(g * K_PASS, D2_PLANE_COLS)
-                u_ps = psum_big.tile([P, K_PASS], F32, tag="big")
-                nc.tensor.matmul_mx(
-                    out=u_ps[:],
-                    lhsT=x_codes[:, bt * P : (bt + 1) * P].bitcast(FP8X4),
-                    lhsT_scale=x_scales[:, bt * P : (bt + 1) * P],
-                    rhs=d2w[:, g * K_PASS : (g + 1) * K_PASS].bitcast(FP8X4),
-                    rhs_scale=d2_scales_sb[4 * plane : P, col : col + K_PASS],
-                    start=True,
-                    stop=True,
-                )
-                nc.scalar.copy(
-                    out=u_tiles[g][:, bt, :, :], in_=u_ps[:].rearrange("b (p t) -> b t p", t=PACK)
-                )
-                nc.vector.bn_stats(out=stats[:, bt, g, :], in_=u_tiles[g][:, bt, :, :])
+        def u_group(bt, g):
+            return u_tiles[bt][g // 2][:, g % 2, :, :]
+
+        def first_product(bt, g):
+            plane, col = divmod(g * K_PASS, D2_PLANE_COLS)
+            c, i = divmod(g, D2_TILE_GROUPS)
+            u_ps = psum_big.tile([P, K_PASS], F32, tag="big")
+            nc.tensor.matmul_mx(
+                out=u_ps[:],
+                lhsT=x_codes[:, bt * P : (bt + 1) * P].bitcast(FP8X4),
+                lhsT_scale=x_scales[:, bt * P : (bt + 1) * P],
+                rhs=d2_tiles[c][:, i * K_PASS : (i + 1) * K_PASS].bitcast(FP8X4),
+                rhs_scale=d2_scales_sb[4 * plane : P, col : col + K_PASS],
+                start=True,
+                stop=True,
+            )
+            return u_ps
+
+        def sorted_by_t(u_ps):
+            return u_ps[:].rearrange("b (p t) -> b t p", t=PACK)
+
+        def copy_out(bt, g):
+            u_ps = first_product(bt, g)
+            nc.scalar.copy(out=u_group(bt, g), in_=sorted_by_t(u_ps))
+
+        def group_statistics(bt, g, u):
+            nc.vector.bn_stats(out=stats[:, bt, g, :], in_=u)
 
         def statistics(bt):
             nc.vector.bn_aggr(
@@ -158,143 +191,197 @@ def tile_autoencoder_pb_k_kernel(
                 out=neg_mean[:, bt : bt + 1], in0=mean_var[:, bt, 0:1], scalar1=-1.0
             )
 
-        def normalise(bt, chunk):
-            for g in range(chunk * CHUNK_GROUPS, (chunk + 1) * CHUNK_GROUPS):
-                nc.gpsimd.tensor_scalar(
-                    out=u_tiles[g][:, bt, :, :],
-                    in0=u_tiles[g][:, bt, :, :],
-                    scalar1=neg_mean[:, bt : bt + 1],
-                    scalar2=rstd[bt][:],
-                    op0=ALU.add,
-                    op1=ALU.mult,
+        def normalise(bt, g):
+            nc.gpsimd.tensor_scalar(
+                out=u_group(bt, g),
+                in0=u_group(bt, g),
+                scalar1=neg_mean[:, bt : bt + 1],
+                scalar2=rstd[bt][:],
+                op0=ALU.add,
+                op1=ALU.mult,
+            )
+
+        def multiply_and_normalise(bt, g):
+            u_ps = first_product(bt, g)
+            nc.vector.tensor_scalar(
+                out=u_group(bt, g),
+                in0=sorted_by_t(u_ps),
+                scalar1=neg_mean[:, bt : bt + 1],
+                scalar2=rstd[bt][:],
+                op0=ALU.add,
+                op1=ALU.mult,
+            )
+
+        gb_sorted = e_pool.tile([P, PACK, P], F32, align_bytes=64, tag="e")
+        gb_cols = const.tile([P, PACK, 2 * GROUPS], F32)
+
+        for g in range(GROUPS):
+            copy_out(0, g)
+            group_statistics(0, g, u_group(0, g))
+            if g == GROUPS // 2:
+                nc.vector.tensor_copy(
+                    out=gb_sorted[:], in_=gb_rows[:].rearrange("r (p t) -> r t p", t=PACK)
                 )
+        gbT_ps = psum_tp.tile([P, PACK, P], F32, tag="tp")
+        for t in range(PACK):
+            nc.tensor.transpose(gbT_ps[:, t, :], gb_sorted[:, t, :], ident[:])
+        statistics(0)
+        nc.vector.tensor_copy(out=gb_cols[:], in_=gbT_ps[:, :, 0 : 2 * GROUPS])
+        for g in range(GROUPS):
+            normalise(0, g)
+        for g in range(KEPT):
+            copy_out(1, g)
 
-        for bt in range(BT):
-            first_product(bt)
-            statistics(bt)
-            normalise(bt, 0)
-
-        for a in range(GROUPS // PLANES):
-            for quad in range(4):
-                nc.sync.dma_start(
-                    out=d3_scales_sb[32 * quad : 32 * quad + 4 * PLANES, a, :].bitcast(I32),
-                    in_=D3_scales[PLANES * a : PLANES * (a + 1), 4 * quad : 4 * quad + 4, :].bitcast(I32),
-                )
-
-        d3_tiles = {}
-
-        def load_d3(chunk):
-            for g in range(chunk * CHUNK_GROUPS, (chunk + 1) * CHUNK_GROUPS):
-                d3w = d3_pool.tile([P, N_OUT], I32, align_bytes=64, tag="d3w", name="d3w%d" % g)
-                nc.sync.dma_start(
-                    out=d3w[:], in_=D3_words[g].rearrange("p n t -> p (n t)").bitcast(I32)
-                )
-                d3_tiles[g] = d3w
-
-        load_d3(0)
-
-        acc = [
-            [psum_big.tile([P, N_TILE], F32, tag="big", name="acc%d_%d" % (bt, nt)) for nt in range(NT)]
-            for bt in range(BT)
-        ]
-        v_tiles = {}
+        zT_tiles = {}
         e_tiles = {}
+        h_tiles = {}
 
-        def transpose_and_scale(g):
-            v_sb = act_pool.tile([P, PACK, BATCH], F32, tag="act", name="v%d" % g)
-            v_tiles[g] = v_sb
-            for half in range(2):
-                zT_ps = psum_tp.tile([P, 2, BATCH], F32, tag="tp")
-                for i in range(2):
-                    for bt in range(BT):
-                        nc.tensor.transpose(
-                            zT_ps[:, i, bt * P : (bt + 1) * P], u_tiles[g][:, bt, 2 * half + i, :], ident[:]
-                        )
-                for i in range(2):
-                    t = 2 * half + i
+        def transpose(bt, pair):
+            for j in range(2):
+                zT_ps = psum_tp.tile([P, PACK, P], F32, tag="tp")
+                zT_tiles[bt, pair, j] = zT_ps
+                for t in range(PACK):
+                    nc.tensor.transpose(zT_ps[:, t, :], u_tiles[bt][pair][:, j, t, :], ident[:])
+
+        def scale(bt, pair):
+            for j in range(2):
+                g = 2 * pair + j
+                for t in range(PACK):
                     nc.vector.tensor_scalar(
-                        out=v_sb[:, t, :],
-                        in0=zT_ps[:, i, :],
+                        out=u_tiles[bt][pair][:, j, t, :],
+                        in0=zT_tiles[bt, pair, j][:, t, :],
                         scalar1=gb_cols[:, t, g : g + 1],
                         scalar2=gb_cols[:, t, GROUPS + g : GROUPS + g + 1],
                         op0=ALU.mult,
                         op1=ALU.add,
                     )
 
-        def prepare(chunk):
-            for g in range(chunk * CHUNK_GROUPS, (chunk + 1) * CHUNK_GROUPS):
-                transpose_and_scale(g)
-
-        def sigmoids(chunk):
-            for g in range(chunk * CHUNK_GROUPS, (chunk + 1) * CHUNK_GROUPS):
-                e_sb = act_pool.tile([P, PACK, BATCH], F32, tag="act", name="e%d" % g)
-                e_tiles[g] = e_sb
-                nc.scalar.activation(out=e_sb[:], in_=v_tiles[g][:], func=ACT.Sigmoid, scale=-1.0)
-
-        def logs(chunk):
-            for g in range(chunk * CHUNK_GROUPS, (chunk + 1) * CHUNK_GROUPS):
-                nc.scalar.activation(out=e_tiles[g][:], in_=e_tiles[g][:], func=ACT.Ln, bias=ln_floor[:])
-
-        h_tiles = {}
-
-        def tanh_and_multiply(g):
-            nc.scalar.activation(out=e_tiles[g][:], in_=e_tiles[g][:], func=ACT.Tanh, scale=-1.0)
-            h_grouped = h_pool.tile([P, BATCH, PACK], BF16, align_bytes=64)
-            h_tiles[g] = h_grouped
-            nc.vector.tensor_tensor(
-                out=h_grouped[:].rearrange("p (c i) t -> p c t i", i=4),
-                in0=v_tiles[g][:].rearrange("p t (c i) -> p c t i", i=4),
-                in1=e_tiles[g][:].rearrange("p t (c i) -> p c t i", i=4),
-                op=ALU.mult,
+        def sigmoid(bt, pair):
+            e_sb = e_pool.tile(
+                [P, 2, PACK, P], F32, align_bytes=64, tag="e", name="e%d_%d" % (bt, pair)
             )
+            e_tiles[bt, pair] = e_sb
+            nc.scalar.activation(out=e_sb[:], in_=u_tiles[bt][pair][:], func=ACT.Sigmoid, scale=-1.0)
 
-        def second_product(g):
-            h_codes = h_pool.tile([P, BATCH], U32, align_bytes=64)
-            h_scales = h_pool.tile([P, BATCH], U8, align_bytes=64)
+        def logs(bt):
+            for pair in range(PAIRS):
+                e_sb = e_tiles[bt, pair]
+                nc.scalar.activation(out=e_sb[:], in_=e_sb[:], func=ACT.Ln, bias=ln_floor[:])
+
+        def tanh(bt, pair):
+            e_sb = e_tiles[bt, pair]
+            nc.scalar.activation(out=e_sb[:], in_=e_sb[:], func=ACT.Tanh, scale=-1.0)
+
+        def multiply(bt, pair):
+            h_grouped = h_pool.tile([P, 2, P, PACK], BF16, align_bytes=64)
+            h_tiles[bt, pair] = h_grouped
+            for j in range(2):
+                nc.vector.tensor_tensor(
+                    out=h_grouped[:, j, :, :].rearrange("p (c i) t -> p c t i", i=4),
+                    in0=u_tiles[bt][pair][:, j, :, :].rearrange("p t (c i) -> p c t i", i=4),
+                    in1=e_tiles[bt, pair][:, j, :, :].rearrange("p t (c i) -> p c t i", i=4),
+                    op=ALU.mult,
+                )
+
+        acc = {}
+
+        def second_product(bt, pair):
+            if pair == 0:
+                for nt in range(NT):
+                    acc[bt, nt] = psum_big.tile(
+                        [P, N_TILE], F32, tag="big", name="acc%d_%d" % (bt, nt)
+                    )
+            h_codes = h_pool.tile([P, 2 * P], U32, align_bytes=64)
+            h_scales = h_pool.tile([P, 2 * P], U8, align_bytes=64)
             nc.vector.quantize_mx(
                 out=h_codes[:].bitcast(FP8X4),
                 scales=h_scales[:],
-                in_=h_tiles[g][:].rearrange("p b t -> p (b t)"),
+                in_=h_tiles[bt, pair][:].rearrange("p j b t -> p (j b t)"),
             )
-            a, k = divmod(g, PLANES)
-            for bt in range(BT):
+            for j in range(2):
+                g = 2 * pair + j
+                a, k = divmod(g, PLANES)
                 for nt in range(NT):
                     nc.tensor.matmul_mx(
-                        out=acc[bt][nt][:],
-                        lhsT=h_codes[:, bt * P : (bt + 1) * P].bitcast(FP8X4),
-                        lhsT_scale=h_scales[:, bt * P : (bt + 1) * P],
+                        out=acc[bt, nt][:],
+                        lhsT=h_codes[:, j * P : (j + 1) * P].bitcast(FP8X4),
+                        lhsT_scale=h_scales[:, j * P : (j + 1) * P],
                         rhs=d3_tiles[g][:, nt * N_TILE : (nt + 1) * N_TILE].bitcast(FP8X4),
                         rhs_scale=d3_scales_sb[4 * k : P, a, nt * N_TILE : (nt + 1) * N_TILE],
                         start=(g == 0),
                         stop=(g == GROUPS - 1),
                     )
 
-        def finish(chunk):
-            first = chunk * CHUNK_GROUPS
-            load_sigmoid_table()
-            for g in range(first, first + CHUNK_GROUPS):
-                tanh_and_multiply(g)
-                if g > first:
-                    second_product(g - 1)
-            second_product(first + CHUNK_GROUPS - 1)
+        y_tiles = {}
 
-        prepare(0)
-        sigmoids(0)
-        for chunk in range(CHUNKS):
-            if chunk + 1 < CHUNKS:
-                for bt in range(BT):
-                    normalise(bt, chunk + 1)
-                prepare(chunk + 1)
-            logs(chunk)
-            finish(chunk)
-            if chunk + 1 < CHUNKS:
-                load_d3(chunk + 1)
-                sigmoids(chunk + 1)
-
-        for bt in range(BT):
+        def add_bias(bt):
             for nt in range(NT):
-                cols = slice(nt * N_TILE, (nt + 1) * N_TILE)
-                y_sb = out_pool.tile([P, N_TILE], F32)
-                nc.vector.tensor_tensor(out=y_sb[:], in0=acc[bt][nt][:], in1=bo_bc[:, cols], op=ALU.add)
+                y_sb = e_pool.tile(
+                    [P, N_TILE], F32, align_bytes=64, tag="e", name="y%d_%d" % (bt, nt)
+                )
+                y_tiles[bt, nt] = y_sb
+                nc.vector.tensor_tensor(
+                    out=y_sb[:],
+                    in0=acc[bt, nt][:],
+                    in1=bo_bc[:, nt * N_TILE : (nt + 1) * N_TILE],
+                    op=ALU.add,
+                )
+
+        def store(bt):
+            for nt in range(NT):
+                y_sb = y_tiles[bt, nt]
                 nc.scalar.activation(out=y_sb[:], in_=y_sb[:], func=ACT.Sigmoid)
-                nc.sync.dma_start(out=out[bt * P : (bt + 1) * P, cols], in_=y_sb[:])
+                nc.sync.dma_start(
+                    out=out[bt * P : (bt + 1) * P, nt * N_TILE : (nt + 1) * N_TILE], in_=y_sb[:]
+                )
+
+        for pair in range(PAIRS):
+            transpose(0, pair)
+            scale(0, pair)
+            sigmoid(0, pair)
+            if pair < KEPT:
+                group_statistics(1, pair, u_group(1, pair))
+        logs(0)
+        for g in range(KEPT, GROUPS):
+            group_statistics(1, g, first_product(1, g)[:])
+        statistics(1)
+        for g in range(KEPT):
+            normalise(1, g)
+
+        load_sigmoid_table()
+        for pair in range(PAIRS):
+            tanh(0, pair)
+        for pair in range(KEPT // 2):
+            multiply_and_normalise(1, KEPT + 2 * pair)
+            multiply_and_normalise(1, KEPT + 2 * pair + 1)
+            transpose(1, pair)
+            scale(1, pair)
+            sigmoid(1, pair)
+
+        load_d3(D3_EARLY, GROUPS)
+        bo_bc = const.tile([P, N_OUT], BF16)
+        nc.sync.dma_start(out=bo_bc[:], in_=bo.partition_broadcast(P))
+
+        for pair in range(PAIRS):
+            multiply(0, pair)
+            late = KEPT // 2 + pair
+            if late < PAIRS:
+                transpose(1, late)
+                scale(1, late)
+                sigmoid(1, late)
+                second_product(0, pair)
+            elif late > PAIRS:
+                second_product(0, pair - 1)
+        second_product(0, PAIRS - 1)
+        add_bias(0)
+        logs(1)
+        load_sigmoid_table()
+        for pair in range(PAIRS):
+            tanh(1, pair)
+            multiply(1, pair)
+            if pair > 0:
+                second_product(1, pair - 1)
+        second_product(1, PAIRS - 1)
+        store(0)
+        add_bias(1)
+        store(1)

@@ -33,7 +33,10 @@ W_BUFS = GROUPS
 D3_EARLY = W_BUFS - D2_TILES
 PAIRS = GROUPS // 2
 E_BUFS = PAIRS + PAIRS // 2
-KEPT = GROUPS // 2
+KEPT_EARLY = 5
+KEPT = 10
+SHARED_PAIRS = (2, 5)
+VECTOR_PAIRS = (0, 4)
 
 FLOPS = 2 * BATCH * K_PASS * FEATS + 2 * BATCH * FEATS * N_OUT
 
@@ -53,7 +56,12 @@ def tile_autoencoder_pb_k_kernel(
         psum_tp = ctx.enter_context(tc.psum_pool(name="psum_tp", bufs=4))
 
         x_sb = e_pool.tile([P, BT, K_PASS], BF16, align_bytes=64, tag="e")
-        nc.sync.dma_start(out=x_sb[:], in_=h_dec1.rearrange("(bt b) k -> b bt k", bt=BT))
+
+        def load_x(bt):
+            nc.sync.dma_start(out=x_sb[:, bt, :], in_=h_dec1[bt * P : (bt + 1) * P, :])
+
+        for bt in range(BT):
+            load_x(bt)
 
         ln_floor = const.tile([P, 1], F32)
         nc.vector.memset(ln_floor[:], LN_FLOOR)
@@ -99,22 +107,27 @@ def tile_autoencoder_pb_k_kernel(
         ident = const.tile([P, P], F32)
         make_identity(nc, ident[:])
 
-        xT_ps = psum_tp.tile([P, BT, 2, P], F32, tag="tp")
-        for bt in range(BT):
-            x_words = x_sb[:, bt, :].bitcast(F32)
-            for u in range(2):
-                nc.tensor.transpose(xT_ps[:, bt, u, :], x_words[:, u : K_PASS // 2 : 2], ident[:])
-        x_grouped = e_pool.tile([P, BATCH * PACK], BF16, align_bytes=64, tag="e")
-        nc.vector.tensor_copy(
-            out=x_grouped[:].bitcast(F32).rearrange("p (bt b u) -> p bt b u", bt=BT, u=2),
-            in_=xT_ps[:].rearrange("p bt u b -> p bt b u"),
-        )
+        x_grouped = e_pool.tile([P, BT, P, PACK], BF16, align_bytes=64, tag="e")
         x_codes = const.tile([P, BATCH], U32, align_bytes=64)
         x_scales = const.tile([P, BATCH], U8, align_bytes=64)
-        nc.vector.quantize_mx(out=x_codes[:].bitcast(FP8X4), scales=x_scales[:], in_=x_grouped[:])
+
+        def prepare_x(bt):
+            rows = slice(bt * P, (bt + 1) * P)
+            x_words = x_sb[:, bt, :].bitcast(F32)
+            xT_ps = psum_tp.tile([P, 2, P], F32, tag="tp")
+            for u in range(2):
+                nc.tensor.transpose(xT_ps[:, u, :], x_words[:, u : K_PASS // 2 : 2], ident[:])
+            x_bt = x_grouped[:, bt, :, :].rearrange("p b t -> p (b t)")
+            nc.vector.tensor_copy(
+                out=x_bt.bitcast(F32).rearrange("p (b u) -> p b u", u=2),
+                in_=xT_ps[:].rearrange("p u b -> p b u"),
+            )
+            nc.vector.quantize_mx(
+                out=x_codes[:, rows].bitcast(FP8X4), scales=x_scales[:, rows], in_=x_bt
+            )
 
         d3_scales_sb = const.tile([P, GROUPS // PLANES, N_OUT], U8, align_bytes=64)
-        nc.vector.memset(d3_scales_sb[:].rearrange("p a n -> p (a n)").bitcast(I32), 0)
+        nc.gpsimd.memset(d3_scales_sb[:].rearrange("p a n -> p (a n)").bitcast(I32), 0)
         for a in range(GROUPS // PLANES):
             for quad in range(4):
                 nc.sync.dma_start(
@@ -191,8 +204,8 @@ def tile_autoencoder_pb_k_kernel(
                 out=neg_mean[:, bt : bt + 1], in0=mean_var[:, bt, 0:1], scalar1=-1.0
             )
 
-        def normalise(bt, g):
-            nc.gpsimd.tensor_scalar(
+        def normalise(engine, bt, g):
+            engine.tensor_scalar(
                 out=u_group(bt, g),
                 in0=u_group(bt, g),
                 scalar1=neg_mean[:, bt : bt + 1],
@@ -213,23 +226,27 @@ def tile_autoencoder_pb_k_kernel(
             )
 
         gb_sorted = e_pool.tile([P, PACK, P], F32, align_bytes=64, tag="e")
+        nc.gpsimd.tensor_copy(out=gb_sorted[:], in_=gb_rows[:].rearrange("r (p t) -> r t p", t=PACK))
         gb_cols = const.tile([P, PACK, 2 * GROUPS], F32)
 
+        prepare_x(0)
         for g in range(GROUPS):
-            copy_out(0, g)
-            group_statistics(0, g, u_group(0, g))
-            if g == GROUPS // 2:
-                nc.vector.tensor_copy(
-                    out=gb_sorted[:], in_=gb_rows[:].rearrange("r (p t) -> r t p", t=PACK)
-                )
+            u_ps = first_product(0, g)
+            if g == 0:
+                prepare_x(1)
+            group_statistics(0, g, u_ps[:])
+            nc.scalar.copy(out=u_group(0, g), in_=sorted_by_t(u_ps))
         gbT_ps = psum_tp.tile([P, PACK, P], F32, tag="tp")
         for t in range(PACK):
             nc.tensor.transpose(gbT_ps[:, t, :], gb_sorted[:, t, :], ident[:])
         statistics(0)
         nc.vector.tensor_copy(out=gb_cols[:], in_=gbT_ps[:, :, 0 : 2 * GROUPS])
         for g in range(GROUPS):
-            normalise(0, g)
-        for g in range(KEPT):
+            if g // 2 not in VECTOR_PAIRS:
+                normalise(nc.gpsimd, 0, g)
+        for g in range(2):
+            normalise(nc.vector, 0, g)
+        for g in range(KEPT_EARLY):
             copy_out(1, g)
 
         zT_tiles = {}
@@ -243,41 +260,52 @@ def tile_autoencoder_pb_k_kernel(
                 for t in range(PACK):
                     nc.tensor.transpose(zT_ps[:, t, :], u_tiles[bt][pair][:, j, t, :], ident[:])
 
-        def scale(bt, pair):
-            for j in range(2):
+        def scale(bt, pair, groups, by_scalar=()):
+            for j in range(groups.start, groups.stop):
                 g = 2 * pair + j
                 for t in range(PACK):
-                    nc.vector.tensor_scalar(
-                        out=u_tiles[bt][pair][:, j, t, :],
-                        in0=zT_tiles[bt, pair, j][:, t, :],
-                        scalar1=gb_cols[:, t, g : g + 1],
-                        scalar2=gb_cols[:, t, GROUPS + g : GROUPS + g + 1],
-                        op0=ALU.mult,
-                        op1=ALU.add,
-                    )
+                    v = u_tiles[bt][pair][:, j, t, :]
+                    zT = zT_tiles[bt, pair, j][:, t, :]
+                    gain = gb_cols[:, t, g : g + 1]
+                    bias = gb_cols[:, t, GROUPS + g : GROUPS + g + 1]
+                    if j in by_scalar:
+                        nc.scalar.activation(
+                            out=v, in_=zT, func=ACT.Identity, scale=gain, bias=bias
+                        )
+                    else:
+                        nc.vector.tensor_scalar(
+                            out=v, in0=zT, scalar1=gain, scalar2=bias, op0=ALU.mult, op1=ALU.add
+                        )
 
-        def sigmoid(bt, pair):
-            e_sb = e_pool.tile(
-                [P, 2, PACK, P], F32, align_bytes=64, tag="e", name="e%d_%d" % (bt, pair)
+        def sigmoid(bt, pair, groups):
+            if groups.start == 0:
+                e_tiles[bt, pair] = e_pool.tile(
+                    [P, 2, PACK, P], F32, align_bytes=64, tag="e", name="e%d_%d" % (bt, pair)
+                )
+            nc.scalar.activation(
+                out=e_tiles[bt, pair][:, groups, :, :],
+                in_=u_tiles[bt][pair][:, groups, :, :],
+                func=ACT.Sigmoid,
+                scale=-1.0,
             )
-            e_tiles[bt, pair] = e_sb
-            nc.scalar.activation(out=e_sb[:], in_=u_tiles[bt][pair][:], func=ACT.Sigmoid, scale=-1.0)
 
         def logs(bt):
             for pair in range(PAIRS):
                 e_sb = e_tiles[bt, pair]
                 nc.scalar.activation(out=e_sb[:], in_=e_sb[:], func=ACT.Ln, bias=ln_floor[:])
 
-        def tanh(bt, pair):
-            e_sb = e_tiles[bt, pair]
-            nc.scalar.activation(out=e_sb[:], in_=e_sb[:], func=ACT.Tanh, scale=-1.0)
+        def tanh(bt, pair, groups):
+            e_sb = e_tiles[bt, pair][:, groups, :, :]
+            nc.scalar.activation(out=e_sb, in_=e_sb, func=ACT.Tanh, scale=-1.0)
 
-        def multiply(bt, pair):
-            h_grouped = h_pool.tile([P, 2, P, PACK], BF16, align_bytes=64)
-            h_tiles[bt, pair] = h_grouped
-            for j in range(2):
+        def multiply(bt, pair, groups):
+            if groups.start == 0:
+                h_tiles[bt, pair] = h_pool.tile(
+                    [P, 2, P, PACK], BF16, align_bytes=64, name="h%d_%d" % (bt, pair), tag="h"
+                )
+            for j in range(groups.start, groups.stop):
                 nc.vector.tensor_tensor(
-                    out=h_grouped[:, j, :, :].rearrange("p (c i) t -> p c t i", i=4),
+                    out=h_tiles[bt, pair][:, j, :, :].rearrange("p (c i) t -> p c t i", i=4),
                     in0=u_tiles[bt][pair][:, j, :, :].rearrange("p t (c i) -> p c t i", i=4),
                     in1=e_tiles[bt, pair][:, j, :, :].rearrange("p t (c i) -> p c t i", i=4),
                     op=ALU.mult,
@@ -285,32 +313,43 @@ def tile_autoencoder_pb_k_kernel(
 
         acc = {}
 
-        def second_product(bt, pair):
-            if pair == 0:
+        codes = {}
+
+        def second_product(bt, pair, groups):
+            if pair == 0 and groups.start == 0:
                 for nt in range(NT):
                     acc[bt, nt] = psum_big.tile(
                         [P, N_TILE], F32, tag="big", name="acc%d_%d" % (bt, nt)
                     )
-            h_codes = h_pool.tile([P, 2 * P], U32, align_bytes=64)
-            h_scales = h_pool.tile([P, 2 * P], U8, align_bytes=64)
+            if groups.start == 0:
+                codes[bt, pair] = (
+                    h_pool.tile([P, 2, P], U32, align_bytes=64, name="hc%d_%d" % (bt, pair), tag="hc"),
+                    h_pool.tile([P, 2, P], U8, align_bytes=64, name="hs%d_%d" % (bt, pair), tag="hs"),
+                )
+            h_codes, h_scales = codes[bt, pair]
             nc.vector.quantize_mx(
-                out=h_codes[:].bitcast(FP8X4),
-                scales=h_scales[:],
-                in_=h_tiles[bt, pair][:].rearrange("p j b t -> p (j b t)"),
+                out=h_codes[:, groups, :].rearrange("p j b -> p (j b)").bitcast(FP8X4),
+                scales=h_scales[:, groups, :].rearrange("p j b -> p (j b)"),
+                in_=h_tiles[bt, pair][:, groups, :, :].rearrange("p j b t -> p (j b t)"),
             )
-            for j in range(2):
+            js = range(groups.start, groups.stop)
+            if pair < PAIRS - 1:
+                order = [(j, nt) for j in js for nt in range(NT)]
+            else:
+                order = [(j, nt) for nt in range(NT) for j in js]
+            for j, nt in order:
                 g = 2 * pair + j
                 a, k = divmod(g, PLANES)
-                for nt in range(NT):
-                    nc.tensor.matmul_mx(
-                        out=acc[bt, nt][:],
-                        lhsT=h_codes[:, j * P : (j + 1) * P].bitcast(FP8X4),
-                        lhsT_scale=h_scales[:, j * P : (j + 1) * P],
-                        rhs=d3_tiles[g][:, nt * N_TILE : (nt + 1) * N_TILE].bitcast(FP8X4),
-                        rhs_scale=d3_scales_sb[4 * k : P, a, nt * N_TILE : (nt + 1) * N_TILE],
-                        start=(g == 0),
-                        stop=(g == GROUPS - 1),
-                    )
+                cols = slice(nt * N_TILE, (nt + 1) * N_TILE)
+                nc.tensor.matmul_mx(
+                    out=acc[bt, nt][:],
+                    lhsT=h_codes[:, j, :].bitcast(FP8X4),
+                    lhsT_scale=h_scales[:, j, :],
+                    rhs=d3_tiles[g][:, cols].bitcast(FP8X4),
+                    rhs_scale=d3_scales_sb[4 * k : P, a, cols],
+                    start=(g == 0),
+                    stop=(g == GROUPS - 1),
+                )
 
         y_tiles = {}
 
@@ -335,53 +374,82 @@ def tile_autoencoder_pb_k_kernel(
                     out=out[bt * P : (bt + 1) * P, nt * N_TILE : (nt + 1) * N_TILE], in_=y_sb[:]
                 )
 
+        BOTH = slice(0, 2)
+        HALVES = [slice(0, 1), slice(1, 2)]
+
+        transpose(0, 0)
         for pair in range(PAIRS):
-            transpose(0, pair)
-            scale(0, pair)
-            sigmoid(0, pair)
-            if pair < KEPT:
-                group_statistics(1, pair, u_group(1, pair))
+            if pair + 1 < PAIRS:
+                if pair + 1 in VECTOR_PAIRS:
+                    for j in range(2):
+                        normalise(nc.vector, 0, 2 * (pair + 1) + j)
+                transpose(0, pair + 1)
+            for groups in HALVES if pair == 0 else [BOTH]:
+                scale(0, pair, groups, by_scalar=(1,) if pair in SHARED_PAIRS else ())
+                sigmoid(0, pair, groups)
+            if KEPT_EARLY + pair < KEPT:
+                copy_out(1, KEPT_EARLY + pair)
         logs(0)
-        for g in range(KEPT, GROUPS):
-            group_statistics(1, g, first_product(1, g)[:])
+        for g in range(GROUPS):
+            group_statistics(1, g, u_group(1, g) if g < KEPT else first_product(1, g)[:])
         statistics(1)
         for g in range(KEPT):
-            normalise(1, g)
+            normalise(nc.gpsimd, 1, g)
 
         load_sigmoid_table()
         for pair in range(PAIRS):
-            tanh(0, pair)
-        for pair in range(KEPT // 2):
-            multiply_and_normalise(1, KEPT + 2 * pair)
-            multiply_and_normalise(1, KEPT + 2 * pair + 1)
-            transpose(1, pair)
-            scale(1, pair)
-            sigmoid(1, pair)
+            tanh(0, pair, BOTH)
+        for pair in range(4):
+            if KEPT + 2 * pair < GROUPS:
+                multiply_and_normalise(1, KEPT + 2 * pair)
+                multiply_and_normalise(1, KEPT + 2 * pair + 1)
+            if pair == 0:
+                transpose(1, 0)
+            transpose(1, pair + 1)
+            scale(1, pair, BOTH)
+            sigmoid(1, pair, BOTH)
 
         load_d3(D3_EARLY, GROUPS)
         bo_bc = const.tile([P, N_OUT], BF16)
         nc.sync.dma_start(out=bo_bc[:], in_=bo.partition_broadcast(P))
 
-        for pair in range(PAIRS):
-            multiply(0, pair)
-            late = KEPT // 2 + pair
-            if late < PAIRS:
-                transpose(1, late)
-                scale(1, late)
-                sigmoid(1, late)
-                second_product(0, pair)
-            elif late > PAIRS:
-                second_product(0, pair - 1)
-        second_product(0, PAIRS - 1)
+        transpose(1, 5)
+        scale(1, 4, BOTH)
+        transpose(1, 6)
+        scale(1, 5, BOTH)
+        transpose(1, 7)
+        multiply(0, 0, BOTH)
+        sigmoid(1, 4, BOTH)
+        multiply(0, 1, BOTH)
+        sigmoid(1, 5, BOTH)
+        second_product(0, 0, BOTH)
+        scale(1, 6, BOTH)
+        multiply(0, 2, BOTH)
+        sigmoid(1, 6, BOTH)
+        second_product(0, 1, BOTH)
+        scale(1, 7, BOTH)
+        multiply(0, 3, BOTH)
+        sigmoid(1, 7, BOTH)
+        second_product(0, 2, BOTH)
+        for pair in range(4, PAIRS):
+            multiply(0, pair, BOTH)
+            second_product(0, pair - 1, BOTH)
+        second_product(0, PAIRS - 1, BOTH)
         add_bias(0)
         logs(1)
         load_sigmoid_table()
+        pending = []
         for pair in range(PAIRS):
-            tanh(1, pair)
-            multiply(1, pair)
-            if pair > 0:
-                second_product(1, pair - 1)
-        second_product(1, PAIRS - 1)
+            for groups in HALVES if pair == 0 else [BOTH]:
+                tanh(1, pair, groups)
+                multiply(1, pair, groups)
+                if pending:
+                    second_product(1, *pending.pop())
+                if pair == 0 and groups.start == 0:
+                    second_product(1, pair, groups)
+                else:
+                    pending.append((pair, groups))
+        second_product(1, *pending.pop())
         store(0)
         add_bias(1)
         store(1)

@@ -32,11 +32,9 @@ D2_TILES = (GROUPS + D2_TILE_GROUPS - 1) // D2_TILE_GROUPS
 W_BUFS = GROUPS
 D3_EARLY = W_BUFS - D2_TILES
 PAIRS = GROUPS // 2
-E_BUFS = PAIRS + PAIRS // 2
-KEPT_EARLY = 5
-KEPT = 10
-SHARED_PAIRS = (2, 5)
-VECTOR_PAIRS = (0, 4)
+E_BUFS = PAIRS + 5
+KEPT_EARLY = 6
+KEPT = 8
 
 FLOPS = 2 * BATCH * K_PASS * FEATS + 2 * BATCH * FEATS * N_OUT
 
@@ -60,8 +58,7 @@ def tile_autoencoder_pb_k_kernel(
         def load_x(bt):
             nc.sync.dma_start(out=x_sb[:, bt, :], in_=h_dec1[bt * P : (bt + 1) * P, :])
 
-        for bt in range(BT):
-            load_x(bt)
+        load_x(0)
 
         ln_floor = const.tile([P, 1], F32)
         nc.vector.memset(ln_floor[:], LN_FLOOR)
@@ -103,6 +100,8 @@ def tile_autoencoder_pb_k_kernel(
                     out=d2w[:, i * K_PASS : (i + 1) * K_PASS],
                     in_=d2_words_i32[:, g * K_PASS : (g + 1) * K_PASS],
                 )
+            if c == 0:
+                load_x(1)
 
         ident = const.tile([P, P], F32)
         make_identity(nc, ident[:])
@@ -232,7 +231,7 @@ def tile_autoencoder_pb_k_kernel(
         prepare_x(0)
         for g in range(GROUPS):
             u_ps = first_product(0, g)
-            if g == 0:
+            if g == GROUPS // 4:
                 prepare_x(1)
             group_statistics(0, g, u_ps[:])
             nc.scalar.copy(out=u_group(0, g), in_=sorted_by_t(u_ps))
@@ -242,12 +241,12 @@ def tile_autoencoder_pb_k_kernel(
         statistics(0)
         nc.vector.tensor_copy(out=gb_cols[:], in_=gbT_ps[:, :, 0 : 2 * GROUPS])
         for g in range(GROUPS):
-            if g // 2 not in VECTOR_PAIRS:
-                normalise(nc.gpsimd, 0, g)
-        for g in range(2):
-            normalise(nc.vector, 0, g)
+            normalise(nc.vector if g < 2 else nc.gpsimd, 0, g)
         for g in range(KEPT_EARLY):
             copy_out(1, g)
+
+        BOTH = slice(0, 2)
+        HALVES = [slice(0, 1), slice(1, 2)]
 
         zT_tiles = {}
         e_tiles = {}
@@ -260,7 +259,7 @@ def tile_autoencoder_pb_k_kernel(
                 for t in range(PACK):
                     nc.tensor.transpose(zT_ps[:, t, :], u_tiles[bt][pair][:, j, t, :], ident[:])
 
-        def scale(bt, pair, groups, by_scalar=()):
+        def scale(bt, pair, groups):
             for j in range(groups.start, groups.stop):
                 g = 2 * pair + j
                 for t in range(PACK):
@@ -268,14 +267,9 @@ def tile_autoencoder_pb_k_kernel(
                     zT = zT_tiles[bt, pair, j][:, t, :]
                     gain = gb_cols[:, t, g : g + 1]
                     bias = gb_cols[:, t, GROUPS + g : GROUPS + g + 1]
-                    if j in by_scalar:
-                        nc.scalar.activation(
-                            out=v, in_=zT, func=ACT.Identity, scale=gain, bias=bias
-                        )
-                    else:
-                        nc.vector.tensor_scalar(
-                            out=v, in0=zT, scalar1=gain, scalar2=bias, op0=ALU.mult, op1=ALU.add
-                        )
+                    nc.vector.tensor_scalar(
+                        out=v, in0=zT, scalar1=gain, scalar2=bias, op0=ALU.mult, op1=ALU.add
+                    )
 
         def sigmoid(bt, pair, groups):
             if groups.start == 0:
@@ -289,39 +283,52 @@ def tile_autoencoder_pb_k_kernel(
                 scale=-1.0,
             )
 
-        def logs(bt):
-            for pair in range(PAIRS):
-                e_sb = e_tiles[bt, pair]
-                nc.scalar.activation(out=e_sb[:], in_=e_sb[:], func=ACT.Ln, bias=ln_floor[:])
+        def logs(bt, pair, groups):
+            e_sb = e_tiles[bt, pair][:, groups, :, :]
+            nc.scalar.activation(out=e_sb, in_=e_sb, func=ACT.Ln, bias=ln_floor[:])
 
         def tanh(bt, pair, groups):
             e_sb = e_tiles[bt, pair][:, groups, :, :]
             nc.scalar.activation(out=e_sb, in_=e_sb, func=ACT.Tanh, scale=-1.0)
 
         def multiply(bt, pair, groups):
-            if groups.start == 0:
+            if (bt, pair) not in h_tiles:
                 h_tiles[bt, pair] = h_pool.tile(
                     [P, 2, P, PACK], BF16, align_bytes=64, name="h%d_%d" % (bt, pair), tag="h"
                 )
             for j in range(groups.start, groups.stop):
-                nc.vector.tensor_tensor(
-                    out=h_tiles[bt, pair][:, j, :, :].rearrange("p (c i) t -> p c t i", i=4),
-                    in0=u_tiles[bt][pair][:, j, :, :].rearrange("p t (c i) -> p c t i", i=4),
-                    in1=e_tiles[bt, pair][:, j, :, :].rearrange("p t (c i) -> p c t i", i=4),
-                    op=ALU.mult,
-                )
+                h = h_tiles[bt, pair][:, j, :, :].rearrange("p (c i) t -> p c t i", i=4)
+                v = u_tiles[bt][pair][:, j, :, :].rearrange("p t (c i) -> p c t i", i=4)
+                e = e_tiles[bt, pair][:, j, :, :].rearrange("p t (c i) -> p c t i", i=4)
+                nc.vector.tensor_tensor(out=h, in0=v, in1=e, op=ALU.mult)
+
+        def square(bt, pair, groups):
+            e_sb = e_tiles[bt, pair][:, groups, :, :]
+            nc.scalar.activation(out=e_sb, in_=e_sb, func=ACT.Square)
+
+        def tanh_by_reciprocal(bt, pair, groups):
+            e_sb = e_tiles[bt, pair][:, groups, :, :]
+            nc.vector.tensor_scalar(
+                out=e_sb, in0=e_sb, scalar1=0.5, scalar2=0.5, op0=ALU.mult, op1=ALU.add
+            )
+            nc.vector.reciprocal(out=e_sb, in_=e_sb)
+            nc.vector.tensor_scalar_add(out=e_sb, in0=e_sb, scalar1=-1.0)
 
         acc = {}
 
         codes = {}
+        LAST = [(PAIRS - 1, BOTH), (PAIRS - 2, BOTH)]
 
         def second_product(bt, pair, groups):
-            if pair == 0 and groups.start == 0:
+            opens = (bt, 0) not in acc
+            if opens:
                 for nt in range(NT):
-                    acc[bt, nt] = psum_big.tile(
-                        [P, N_TILE], F32, tag="big", name="acc%d_%d" % (bt, nt)
+                    acc[bt, nt] = (
+                        psum_big.tile([P, N_TILE], F32, tag="big", name="acc0_%d" % nt)
+                        if bt == 0
+                        else psum_tp.tile([P, N_TILE], F32, tag="tp", name="acc1_%d" % nt)
                     )
-            if groups.start == 0:
+            if (bt, pair) not in codes:
                 codes[bt, pair] = (
                     h_pool.tile([P, 2, P], U32, align_bytes=64, name="hc%d_%d" % (bt, pair), tag="hc"),
                     h_pool.tile([P, 2, P], U8, align_bytes=64, name="hs%d_%d" % (bt, pair), tag="hs"),
@@ -333,7 +340,8 @@ def tile_autoencoder_pb_k_kernel(
                 in_=h_tiles[bt, pair][:, groups, :, :].rearrange("p j b t -> p (j b t)"),
             )
             js = range(groups.start, groups.stop)
-            if pair < PAIRS - 1:
+            closes = (pair, groups) == LAST[bt]
+            if not closes:
                 order = [(j, nt) for j in js for nt in range(NT)]
             else:
                 order = [(j, nt) for nt in range(NT) for j in js]
@@ -347,8 +355,8 @@ def tile_autoencoder_pb_k_kernel(
                     lhsT_scale=h_scales[:, j, :],
                     rhs=d3_tiles[g][:, cols].bitcast(FP8X4),
                     rhs_scale=d3_scales_sb[4 * k : P, a, cols],
-                    start=(g == 0),
-                    stop=(g == GROUPS - 1),
+                    start=opens and j == groups.start,
+                    stop=closes and j == groups.stop - 1,
                 )
 
         y_tiles = {}
@@ -374,22 +382,17 @@ def tile_autoencoder_pb_k_kernel(
                     out=out[bt * P : (bt + 1) * P, nt * N_TILE : (nt + 1) * N_TILE], in_=y_sb[:]
                 )
 
-        BOTH = slice(0, 2)
-        HALVES = [slice(0, 1), slice(1, 2)]
-
         transpose(0, 0)
         for pair in range(PAIRS):
             if pair + 1 < PAIRS:
-                if pair + 1 in VECTOR_PAIRS:
-                    for j in range(2):
-                        normalise(nc.vector, 0, 2 * (pair + 1) + j)
                 transpose(0, pair + 1)
             for groups in HALVES if pair == 0 else [BOTH]:
-                scale(0, pair, groups, by_scalar=(1,) if pair in SHARED_PAIRS else ())
+                scale(0, pair, groups)
                 sigmoid(0, pair, groups)
             if KEPT_EARLY + pair < KEPT:
                 copy_out(1, KEPT_EARLY + pair)
-        logs(0)
+        for pair in range(PAIRS):
+            logs(0, pair, BOTH)
         for g in range(GROUPS):
             group_statistics(1, g, u_group(1, g) if g < KEPT else first_product(1, g)[:])
         statistics(1)
@@ -415,41 +418,45 @@ def tile_autoencoder_pb_k_kernel(
 
         transpose(1, 5)
         scale(1, 4, BOTH)
+        sigmoid(1, 4, BOTH)
         transpose(1, 6)
         scale(1, 5, BOTH)
         transpose(1, 7)
         multiply(0, 0, BOTH)
-        sigmoid(1, 4, BOTH)
-        multiply(0, 1, BOTH)
         sigmoid(1, 5, BOTH)
-        second_product(0, 0, BOTH)
         scale(1, 6, BOTH)
-        multiply(0, 2, BOTH)
+        second_product(0, 0, BOTH)
+        multiply(0, 1, BOTH)
         sigmoid(1, 6, BOTH)
-        second_product(0, 1, BOTH)
         scale(1, 7, BOTH)
-        multiply(0, 3, BOTH)
+        second_product(0, 1, BOTH)
+        multiply(0, 2, BOTH)
         sigmoid(1, 7, BOTH)
+        square(1, 7, HALVES[1])
+        multiply(0, 3, BOTH)
         second_product(0, 2, BOTH)
         for pair in range(4, PAIRS):
             multiply(0, pair, BOTH)
             second_product(0, pair - 1, BOTH)
         second_product(0, PAIRS - 1, BOTH)
+        tanh_by_reciprocal(1, PAIRS - 1, HALVES[1])
         add_bias(0)
-        logs(1)
+        multiply(1, PAIRS - 1, HALVES[1])
+        second_product(1, PAIRS - 1, HALVES[1])
+        for pair in range(PAIRS - 1):
+            logs(1, pair, BOTH)
+        logs(1, PAIRS - 1, HALVES[0])
         load_sigmoid_table()
-        pending = []
-        for pair in range(PAIRS):
-            for groups in HALVES if pair == 0 else [BOTH]:
-                tanh(1, pair, groups)
-                multiply(1, pair, groups)
-                if pending:
-                    second_product(1, *pending.pop())
-                if pair == 0 and groups.start == 0:
-                    second_product(1, pair, groups)
-                else:
-                    pending.append((pair, groups))
-        second_product(1, *pending.pop())
+        steps = [(0, HALVES[0]), (0, HALVES[1])] + [(pair, BOTH) for pair in range(1, PAIRS - 2)]
+        steps += [(PAIRS - 1, HALVES[0]), (PAIRS - 2, BOTH)]
+        for i, (pair, groups) in enumerate(steps):
+            tanh(1, pair, groups)
+            multiply(1, pair, groups)
+            if i > 1:
+                second_product(1, *steps[i - 1])
+            if i == 0:
+                second_product(1, pair, groups)
+        second_product(1, *steps[-1])
         store(0)
         add_bias(1)
         store(1)

@@ -34,7 +34,8 @@ D3_EARLY = W_BUFS - D2_TILES
 PAIRS = GROUPS // 2
 E_BUFS = PAIRS + 5
 KEPT_EARLY = 6
-KEPT = 8
+KEPT = 10
+GPSIMD_PAIRS = 3
 
 FLOPS = 2 * BATCH * K_PASS * FEATS + 2 * BATCH * FEATS * N_OUT
 
@@ -300,24 +301,12 @@ def tile_autoencoder_pb_k_kernel(
                 h = h_tiles[bt, pair][:, j, :, :].rearrange("p (c i) t -> p c t i", i=4)
                 v = u_tiles[bt][pair][:, j, :, :].rearrange("p t (c i) -> p c t i", i=4)
                 e = e_tiles[bt, pair][:, j, :, :].rearrange("p t (c i) -> p c t i", i=4)
-                nc.vector.tensor_tensor(out=h, in0=v, in1=e, op=ALU.mult)
-
-        def square(bt, pair, groups):
-            e_sb = e_tiles[bt, pair][:, groups, :, :]
-            nc.scalar.activation(out=e_sb, in_=e_sb, func=ACT.Square)
-
-        def tanh_by_reciprocal(bt, pair, groups):
-            e_sb = e_tiles[bt, pair][:, groups, :, :]
-            nc.vector.tensor_scalar(
-                out=e_sb, in0=e_sb, scalar1=0.5, scalar2=0.5, op0=ALU.mult, op1=ALU.add
-            )
-            nc.vector.reciprocal(out=e_sb, in_=e_sb)
-            nc.vector.tensor_scalar_add(out=e_sb, in0=e_sb, scalar1=-1.0)
+                engine = nc.gpsimd if bt == 0 and pair < GPSIMD_PAIRS else nc.vector
+                engine.tensor_tensor(out=h, in0=v, in1=e, op=ALU.mult)
 
         acc = {}
 
         codes = {}
-        LAST = [(PAIRS - 1, BOTH), (PAIRS - 2, BOTH)]
 
         def second_product(bt, pair, groups):
             opens = (bt, 0) not in acc
@@ -340,7 +329,7 @@ def tile_autoencoder_pb_k_kernel(
                 in_=h_tiles[bt, pair][:, groups, :, :].rearrange("p j b t -> p (j b t)"),
             )
             js = range(groups.start, groups.stop)
-            closes = (pair, groups) == LAST[bt]
+            closes = pair == PAIRS - 1
             if not closes:
                 order = [(j, nt) for j in js for nt in range(NT)]
             else:
@@ -395,6 +384,7 @@ def tile_autoencoder_pb_k_kernel(
             logs(0, pair, BOTH)
         for g in range(GROUPS):
             group_statistics(1, g, u_group(1, g) if g < KEPT else first_product(1, g)[:])
+        load_d3(D3_EARLY, D3_EARLY + KEPT // D2_TILE_GROUPS)
         statistics(1)
         for g in range(KEPT):
             normalise(nc.gpsimd, 1, g)
@@ -412,43 +402,37 @@ def tile_autoencoder_pb_k_kernel(
             scale(1, pair, BOTH)
             sigmoid(1, pair, BOTH)
 
-        load_d3(D3_EARLY, GROUPS)
+        load_d3(D3_EARLY + KEPT // D2_TILE_GROUPS, GROUPS)
         bo_bc = const.tile([P, N_OUT], BF16)
         nc.sync.dma_start(out=bo_bc[:], in_=bo.partition_broadcast(P))
 
         transpose(1, 5)
         scale(1, 4, BOTH)
         sigmoid(1, 4, BOTH)
+        multiply(0, 0, BOTH)
         transpose(1, 6)
         scale(1, 5, BOTH)
-        transpose(1, 7)
-        multiply(0, 0, BOTH)
         sigmoid(1, 5, BOTH)
-        scale(1, 6, BOTH)
-        second_product(0, 0, BOTH)
+        transpose(1, 7)
         multiply(0, 1, BOTH)
+        scale(1, 6, BOTH)
         sigmoid(1, 6, BOTH)
-        scale(1, 7, BOTH)
-        second_product(0, 1, BOTH)
+        second_product(0, 0, BOTH)
         multiply(0, 2, BOTH)
+        scale(1, 7, BOTH)
         sigmoid(1, 7, BOTH)
-        square(1, 7, HALVES[1])
+        second_product(0, 1, BOTH)
         multiply(0, 3, BOTH)
         second_product(0, 2, BOTH)
         for pair in range(4, PAIRS):
             multiply(0, pair, BOTH)
             second_product(0, pair - 1, BOTH)
         second_product(0, PAIRS - 1, BOTH)
-        tanh_by_reciprocal(1, PAIRS - 1, HALVES[1])
         add_bias(0)
-        multiply(1, PAIRS - 1, HALVES[1])
-        second_product(1, PAIRS - 1, HALVES[1])
-        for pair in range(PAIRS - 1):
+        for pair in range(PAIRS):
             logs(1, pair, BOTH)
-        logs(1, PAIRS - 1, HALVES[0])
         load_sigmoid_table()
-        steps = [(0, HALVES[0]), (0, HALVES[1])] + [(pair, BOTH) for pair in range(1, PAIRS - 2)]
-        steps += [(PAIRS - 1, HALVES[0]), (PAIRS - 2, BOTH)]
+        steps = [(0, HALVES[0]), (0, HALVES[1])] + [(pair, BOTH) for pair in range(1, PAIRS)]
         for i, (pair, groups) in enumerate(steps):
             tanh(1, pair, groups)
             multiply(1, pair, groups)

@@ -33,8 +33,8 @@ W_BUFS = GROUPS
 D3_EARLY = W_BUFS - D2_TILES
 PAIRS = GROUPS // 2
 E_BUFS = PAIRS + 5
-KEPT_EARLY = 6
-KEPT = 10
+KEPT_EARLY = 2
+KEPT = 8
 GPSIMD_PAIRS = 3
 
 FLOPS = 2 * BATCH * K_PASS * FEATS + 2 * BATCH * FEATS * N_OUT
@@ -232,8 +232,6 @@ def tile_autoencoder_pb_k_kernel(
         prepare_x(0)
         for g in range(GROUPS):
             u_ps = first_product(0, g)
-            if g == GROUPS // 4:
-                prepare_x(1)
             group_statistics(0, g, u_ps[:])
             nc.scalar.copy(out=u_group(0, g), in_=sorted_by_t(u_ps))
         gbT_ps = psum_tp.tile([P, PACK, P], F32, tag="tp")
@@ -241,6 +239,7 @@ def tile_autoencoder_pb_k_kernel(
             nc.tensor.transpose(gbT_ps[:, t, :], gb_sorted[:, t, :], ident[:])
         statistics(0)
         nc.vector.tensor_copy(out=gb_cols[:], in_=gbT_ps[:, :, 0 : 2 * GROUPS])
+        prepare_x(1)
         for g in range(GROUPS):
             normalise(nc.vector if g < 2 else nc.gpsimd, 0, g)
         for g in range(KEPT_EARLY):
@@ -350,25 +349,31 @@ def tile_autoencoder_pb_k_kernel(
 
         y_tiles = {}
 
+        pieces = [
+            [(nt, 0, N_TILE) for nt in range(NT)],
+            [(nt, 0, N_TILE) for nt in range(NT - 1)]
+            + [(NT - 1, 0, N_TILE // 2), (NT - 1, N_TILE // 2, N_TILE)],
+        ]
+
         def add_bias(bt):
-            for nt in range(NT):
-                y_sb = e_pool.tile(
-                    [P, N_TILE], F32, align_bytes=64, tag="e", name="y%d_%d" % (bt, nt)
-                )
-                y_tiles[bt, nt] = y_sb
+            for nt, first, last in pieces[bt]:
+                if first == 0:
+                    y_tiles[bt, nt] = e_pool.tile(
+                        [P, N_TILE], F32, align_bytes=64, tag="e", name="y%d_%d" % (bt, nt)
+                    )
                 nc.vector.tensor_tensor(
-                    out=y_sb[:],
-                    in0=acc[bt, nt][:],
-                    in1=bo_bc[:, nt * N_TILE : (nt + 1) * N_TILE],
+                    out=y_tiles[bt, nt][:, first:last],
+                    in0=acc[bt, nt][:, first:last],
+                    in1=bo_bc[:, nt * N_TILE + first : nt * N_TILE + last],
                     op=ALU.add,
                 )
 
         def store(bt):
-            for nt in range(NT):
-                y_sb = y_tiles[bt, nt]
-                nc.scalar.activation(out=y_sb[:], in_=y_sb[:], func=ACT.Sigmoid)
+            for nt, first, last in pieces[bt]:
+                y = y_tiles[bt, nt][:, first:last]
+                nc.scalar.activation(out=y, in_=y, func=ACT.Sigmoid)
                 nc.sync.dma_start(
-                    out=out[bt * P : (bt + 1) * P, nt * N_TILE : (nt + 1) * N_TILE], in_=y_sb[:]
+                    out=out[bt * P : (bt + 1) * P, nt * N_TILE + first : nt * N_TILE + last], in_=y
                 )
 
         transpose(0, 0)
@@ -429,10 +434,11 @@ def tile_autoencoder_pb_k_kernel(
             second_product(0, pair - 1, BOTH)
         second_product(0, PAIRS - 1, BOTH)
         add_bias(0)
-        for pair in range(PAIRS):
+        last = PAIRS - 1
+        steps = [(0, HALVES[0]), (0, HALVES[1])] + [(pair, BOTH) for pair in range(1, last)]
+        for pair in range(last):
             logs(1, pair, BOTH)
         load_sigmoid_table()
-        steps = [(0, HALVES[0]), (0, HALVES[1])] + [(pair, BOTH) for pair in range(1, PAIRS)]
         for i, (pair, groups) in enumerate(steps):
             tanh(1, pair, groups)
             multiply(1, pair, groups)
@@ -441,6 +447,12 @@ def tile_autoencoder_pb_k_kernel(
             if i == 0:
                 second_product(1, pair, groups)
         second_product(1, *steps[-1])
+        logs(1, last, BOTH)
+        load_sigmoid_table()
+        for groups in HALVES:
+            tanh(1, last, groups)
+            multiply(1, last, groups)
+        second_product(1, last, BOTH)
         store(0)
         add_bias(1)
         store(1)

@@ -34,7 +34,7 @@ D3_EARLY = W_BUFS - D2_TILES
 PAIRS = GROUPS // 2
 E_BUFS = PAIRS + 5
 KEPT_EARLY = 2
-KEPT = 8
+KEPT = 4
 GPSIMD_PAIRS = 3
 
 FLOPS = 2 * BATCH * K_PASS * FEATS + 2 * BATCH * FEATS * N_OUT
@@ -397,43 +397,36 @@ def tile_autoencoder_pb_k_kernel(
         load_sigmoid_table()
         for pair in range(PAIRS):
             tanh(0, pair, BOTH)
+        again = list(range(KEPT, GROUPS))
         for pair in range(4):
-            if KEPT + 2 * pair < GROUPS:
-                multiply_and_normalise(1, KEPT + 2 * pair)
-                multiply_and_normalise(1, KEPT + 2 * pair + 1)
+            for g in again[3 * pair : 3 * pair + 3]:
+                multiply_and_normalise(1, g)
+                if (g + 1) % D2_TILE_GROUPS == 0 or g + 1 == GROUPS:
+                    load_d3(len(d3_tiles), len(d3_tiles) + 1)
             if pair == 0:
                 transpose(1, 0)
             transpose(1, pair + 1)
             scale(1, pair, BOTH)
             sigmoid(1, pair, BOTH)
 
-        load_d3(D3_EARLY + KEPT // D2_TILE_GROUPS, GROUPS)
         bo_bc = const.tile([P, N_OUT], BF16)
         nc.sync.dma_start(out=bo_bc[:], in_=bo.partition_broadcast(P))
 
         transpose(1, 5)
         scale(1, 4, BOTH)
         sigmoid(1, 4, BOTH)
-        multiply(0, 0, BOTH)
-        transpose(1, 6)
-        scale(1, 5, BOTH)
-        sigmoid(1, 5, BOTH)
-        transpose(1, 7)
-        multiply(0, 1, BOTH)
-        scale(1, 6, BOTH)
-        sigmoid(1, 6, BOTH)
-        second_product(0, 0, BOTH)
-        multiply(0, 2, BOTH)
-        scale(1, 7, BOTH)
-        sigmoid(1, 7, BOTH)
-        second_product(0, 1, BOTH)
-        multiply(0, 3, BOTH)
-        second_product(0, 2, BOTH)
-        for pair in range(4, PAIRS):
+        for pair in range(5, PAIRS):
+            if pair + 1 < PAIRS:
+                transpose(1, pair + 1)
+            scale(1, pair, BOTH)
+            multiply(0, pair - 5, BOTH)
+            sigmoid(1, pair, BOTH)
+        for pair in range(3, PAIRS):
+            second_product(0, pair - 3, BOTH)
             multiply(0, pair, BOTH)
-            second_product(0, pair - 1, BOTH)
+        for pair in range(PAIRS - 3, PAIRS - 1):
+            second_product(0, pair, BOTH)
         second_product(0, PAIRS - 1, BOTH)
-        add_bias(0)
         last = PAIRS - 1
         steps = [(0, HALVES[0]), (0, HALVES[1])] + [(pair, BOTH) for pair in range(1, last)]
         for pair in range(last):
@@ -447,6 +440,7 @@ def tile_autoencoder_pb_k_kernel(
             if i == 0:
                 second_product(1, pair, groups)
         second_product(1, *steps[-1])
+        add_bias(0)
         logs(1, last, BOTH)
         load_sigmoid_table()
         for groups in HALVES:

@@ -101,8 +101,7 @@ def tile_autoencoder_pb_k_kernel(
                     out=d2w[:, i * K_PASS : (i + 1) * K_PASS],
                     in_=d2_words_i32[:, g * K_PASS : (g + 1) * K_PASS],
                 )
-            if c == 0:
-                load_x(1)
+        load_x(1)
 
         ident = const.tile([P, P], F32)
         make_identity(nc, ident[:])
@@ -240,8 +239,22 @@ def tile_autoencoder_pb_k_kernel(
         statistics(0)
         nc.vector.tensor_copy(out=gb_cols[:], in_=gbT_ps[:, :, 0 : 2 * GROUPS])
         prepare_x(1)
-        for g in range(GROUPS):
-            normalise(nc.vector if g < 2 else nc.gpsimd, 0, g)
+        shift = const.tile([P, 1], F32)
+        nc.vector.tensor_tensor(
+            out=shift[:], in0=neg_mean[:, 0:1], in1=rstd[0][:], op=ALU.mult
+        )
+        for g in range(2):
+            normalise(nc.vector, 0, g)
+        for g in range(2, 4):
+            nc.scalar.activation(
+                out=u_group(0, g),
+                in_=u_group(0, g),
+                func=ACT.Identity,
+                scale=rstd[0][:],
+                bias=shift[:],
+            )
+        for g in range(4, GROUPS):
+            normalise(nc.gpsimd, 0, g)
         for g in range(KEPT_EARLY):
             copy_out(1, g)
 

from contextlib import ExitStack

import concourse.mybir as mybir
from concourse.masks import make_identity

F32 = mybir.dt.float32
BF16 = mybir.dt.bfloat16
I32 = mybir.dt.int32
U32 = mybir.dt.uint32
U8 = mybir.dt.uint8
FP8X4 = mybir.dt.float8_e4m3fn_x4
ACT = mybir.ActivationFunctionType
ALU = mybir.AluOpType

P = 128
PACK = 4
K_PASS = P * PACK
BATCH = 256
BT = BATCH // P
FEATS = 8192
GROUPS = FEATS // K_PASS
N_OUT = 1536
N_TILE = 512
NT = N_OUT // N_TILE
EPS = 1e-5
LN_FLOOR = 2.0 ** -60

PLANES = 4
D2_PLANE_COLS = FEATS // PLANES
D2_TILE_GROUPS = N_OUT // K_PASS
D2_TILES = (GROUPS + D2_TILE_GROUPS - 1) // D2_TILE_GROUPS
W_BUFS = GROUPS
D3_EARLY = W_BUFS - D2_TILES
PAIRS = GROUPS // 2
E_BUFS = PAIRS + 5
KEPT_EARLY = 2
KEPT = 4
GPSIMD_PAIRS = 3

FLOPS = 2 * BATCH * K_PASS * FEATS + 2 * BATCH * FEATS * N_OUT


def tile_autoencoder_pb_k_kernel(
    tc, h_dec1, D2_words, D2_scales, g4, b4, D3_words, D3_scales, bo, out
):
    nc = tc.nc
    with ExitStack() as ctx:
        ctx.enter_context(tc.manual_schedule())
        const = ctx.enter_context(tc.tile_pool(name="const", bufs=1))
        w_pool = ctx.enter_context(tc.tile_pool(name="weights", bufs=W_BUFS))
        u_pool = ctx.enter_context(tc.tile_pool(name="u", bufs=BT * PAIRS))
        e_pool = ctx.enter_context(tc.tile_pool(name="e", bufs=E_BUFS))
        h_pool = ctx.enter_context(tc.tile_pool(name="h", bufs=3))
        psum_big = ctx.enter_context(tc.psum_pool(name="psum_big", bufs=4))
        psum_tp = ctx.enter_context(tc.psum_pool(name="psum_tp", bufs=4))

        x_sb = e_pool.tile([P, BT, K_PASS], BF16, align_bytes=64, tag="e")

        def load_x(bt):
            nc.sync.dma_start(out=x_sb[:, bt, :], in_=h_dec1[bt * P : (bt + 1) * P, :])

        load_x(0)

        ln_floor = const.tile([P, 1], F32)
        nc.vector.memset(ln_floor[:], LN_FLOOR)
        neg_half = const.tile([P, 1], F32)
        nc.vector.memset(neg_half[:], -0.5)

        d2_scales_sb = const.tile([P, D2_PLANE_COLS], U8, align_bytes=64)
        nc.vector.memset(d2_scales_sb[:].bitcast(I32), 0)
        for quad in range(4):
            nc.sync.dma_start(
                out=d2_scales_sb[32 * quad : 32 * quad + 4 * PLANES, :].bitcast(I32),
                in_=D2_scales[0, 4 * quad : 4 * quad + 4, :]
                .rearrange("r (k n) -> k r n", k=PLANES)
                .bitcast(I32),
            )

        warm = const.tile([P, 1], F32)

        def load_sigmoid_table():
            nc.scalar.activation(out=warm[:], in_=ln_floor[:], func=ACT.Sigmoid)

        load_sigmoid_table()

        gb_rows = e_pool.tile([P, K_PASS], BF16, align_bytes=64, tag="e")
        nc.vector.memset(gb_rows[:], 0.0)
        nc.scalar.dma_start(out=gb_rows[0:GROUPS, :], in_=g4.rearrange("(g k) -> g k", k=K_PASS))
        nc.scalar.dma_start(
            out=gb_rows[GROUPS : 2 * GROUPS, :], in_=b4.rearrange("(g k) -> g k", k=K_PASS)
        )

        d2_words_i32 = D2_words[0].rearrange("p n t -> p (n t)").bitcast(I32)
        d2_tiles = []
        for c in range(D2_TILES):
            d2w = w_pool.tile([P, N_OUT], I32, align_bytes=64, tag="w", name="d2w%d" % c)
            d2_tiles.append(d2w)
            for i in range(min(D2_TILE_GROUPS, GROUPS - c * D2_TILE_GROUPS)):
                g = c * D2_TILE_GROUPS + i
                nc.sync.dma_start(
                    out=d2w[:, i * K_PASS : (i + 1) * K_PASS],
                    in_=d2_words_i32[:, g * K_PASS : (g + 1) * K_PASS],
                )
        load_x(1)

        ident = const.tile([P, P], F32)
        make_identity(nc, ident[:])

        x_grouped = e_pool.tile([P, BT, P, PACK], BF16, align_bytes=64, tag="e")
        x_codes = const.tile([P, BATCH], U32, align_bytes=64)
        x_scales = const.tile([P, BATCH], U8, align_bytes=64)

        def prepare_x(bt):
            rows = slice(bt * P, (bt + 1) * P)
            x_words = x_sb[:, bt, :].bitcast(F32)
            xT_ps = psum_tp.tile([P, 2, P], F32, tag="tp")
            for u in range(2):
                nc.tensor.transpose(xT_ps[:, u, :], x_words[:, u : K_PASS // 2 : 2], ident[:])
            x_bt = x_grouped[:, bt, :, :].rearrange("p b t -> p (b t)")
            nc.vector.tensor_copy(
                out=x_bt.bitcast(F32).rearrange("p (b u) -> p b u", u=2),
                in_=xT_ps[:].rearrange("p u b -> p b u"),
            )
            nc.vector.quantize_mx(
                out=x_codes[:, rows].bitcast(FP8X4), scales=x_scales[:, rows], in_=x_bt
            )

        d3_scales_sb = const.tile([P, GROUPS // PLANES, N_OUT], U8, align_bytes=64)
        nc.gpsimd.memset(d3_scales_sb[:].rearrange("p a n -> p (a n)").bitcast(I32), 0)
        for a in range(GROUPS // PLANES):
            for quad in range(4):
                nc.sync.dma_start(
                    out=d3_scales_sb[32 * quad : 32 * quad + 4 * PLANES, a, :].bitcast(I32),
                    in_=D3_scales[PLANES * a : PLANES * (a + 1), 4 * quad : 4 * quad + 4, :].bitcast(I32),
                )

        d3_tiles = []

        def load_d3(first, last):
            for g in range(first, last):
                d3w = w_pool.tile([P, N_OUT], I32, align_bytes=64, tag="w", name="d3w%d" % g)
                nc.sync.dma_start(
                    out=d3w[:], in_=D3_words[g].rearrange("p n t -> p (n t)").bitcast(I32)
                )
                d3_tiles.append(d3w)

        load_d3(0, D3_EARLY)

        u_tiles = [
            [
                u_pool.tile(
                    [P, 2, PACK, P], F32, align_bytes=64, tag="u", name="u%d_%d" % (bt, pair)
                )
                for pair in range(PAIRS)
            ]
            for bt in range(BT)
        ]
        stats = const.tile([P, BT, GROUPS, 6], F32)
        mean_var = const.tile([P, BT, 2], F32)
        neg_mean = const.tile([P, BT], F32)
        var_eps = const.tile([P, BT], F32)
        rstd = [const.tile([P, 1], F32, name="rstd%d" % bt) for bt in range(BT)]

        def u_group(bt, g):
            return u_tiles[bt][g // 2][:, g % 2, :, :]

        def first_product(bt, g):
            plane, col = divmod(g * K_PASS, D2_PLANE_COLS)
            c, i = divmod(g, D2_TILE_GROUPS)
            u_ps = psum_big.tile([P, K_PASS], F32, tag="big")
            nc.tensor.matmul_mx(
                out=u_ps[:],
                lhsT=x_codes[:, bt * P : (bt + 1) * P].bitcast(FP8X4),
                lhsT_scale=x_scales[:, bt * P : (bt + 1) * P],
                rhs=d2_tiles[c][:, i * K_PASS : (i + 1) * K_PASS].bitcast(FP8X4),
                rhs_scale=d2_scales_sb[4 * plane : P, col : col + K_PASS],
                start=True,
                stop=True,
            )
            return u_ps

        def sorted_by_t(u_ps):
            return u_ps[:].rearrange("b (p t) -> b t p", t=PACK)

        def copy_out(bt, g):
            u_ps = first_product(bt, g)
            nc.scalar.copy(out=u_group(bt, g), in_=sorted_by_t(u_ps))

        def group_statistics(bt, g, u):
            nc.vector.bn_stats(out=stats[:, bt, g, :], in_=u)

        def statistics(bt):
            nc.vector.bn_aggr(
                out=mean_var[:, bt, :], in_=stats[:, bt, :, :].rearrange("p g s -> p (g s)")
            )
            nc.vector.tensor_scalar_add(
                out=var_eps[:, bt : bt + 1], in0=mean_var[:, bt, 1:2], scalar1=EPS
            )
            nc.gpsimd.tensor_tensor(
                out=rstd[bt][:], in0=var_eps[:, bt : bt + 1], in1=neg_half[:], op=ALU.pow
            )
            nc.vector.tensor_scalar_mul(
                out=neg_mean[:, bt : bt + 1], in0=mean_var[:, bt, 0:1], scalar1=-1.0
            )

        def normalise(engine, bt, g):
            engine.tensor_scalar(
                out=u_group(bt, g),
                in0=u_group(bt, g),
                scalar1=neg_mean[:, bt : bt + 1],
                scalar2=rstd[bt][:],
                op0=ALU.add,
                op1=ALU.mult,
            )

        def multiply_and_normalise(bt, g):
            u_ps = first_product(bt, g)
            nc.vector.tensor_scalar(
                out=u_group(bt, g),
                in0=sorted_by_t(u_ps),
                scalar1=neg_mean[:, bt : bt + 1],
                scalar2=rstd[bt][:],
                op0=ALU.add,
                op1=ALU.mult,
            )

        gb_sorted = e_pool.tile([P, PACK, P], F32, align_bytes=64, tag="e")
        nc.gpsimd.tensor_copy(out=gb_sorted[:], in_=gb_rows[:].rearrange("r (p t) -> r t p", t=PACK))
        gb_cols = const.tile([P, PACK, 2 * GROUPS], F32)

        prepare_x(0)
        for g in range(GROUPS):
            u_ps = first_product(0, g)
            group_statistics(0, g, u_ps[:])
            nc.scalar.copy(out=u_group(0, g), in_=sorted_by_t(u_ps))
        gbT_ps = psum_tp.tile([P, PACK, P], F32, tag="tp")
        for t in range(PACK):
            nc.tensor.transpose(gbT_ps[:, t, :], gb_sorted[:, t, :], ident[:])
        statistics(0)
        nc.vector.tensor_copy(out=gb_cols[:], in_=gbT_ps[:, :, 0 : 2 * GROUPS])
        prepare_x(1)
        shift = const.tile([P, 1], F32)
        nc.vector.tensor_tensor(
            out=shift[:], in0=neg_mean[:, 0:1], in1=rstd[0][:], op=ALU.mult
        )
        for g in range(2):
            normalise(nc.vector, 0, g)
        for g in range(2, 4):
            nc.scalar.activation(
                out=u_group(0, g),
                in_=u_group(0, g),
                func=ACT.Identity,
                scale=rstd[0][:],
                bias=shift[:],
            )
        for g in range(4, GROUPS):
            normalise(nc.gpsimd, 0, g)
        for g in range(KEPT_EARLY):
            copy_out(1, g)

        BOTH = slice(0, 2)
        HALVES = [slice(0, 1), slice(1, 2)]

        zT_tiles = {}
        e_tiles = {}
        h_tiles = {}

        def transpose(bt, pair):
            for j in range(2):
                zT_ps = psum_tp.tile([P, PACK, P], F32, tag="tp")
                zT_tiles[bt, pair, j] = zT_ps
                for t in range(PACK):
                    nc.tensor.transpose(zT_ps[:, t, :], u_tiles[bt][pair][:, j, t, :], ident[:])

        def scale(bt, pair, groups):
            for j in range(groups.start, groups.stop):
                g = 2 * pair + j
                for t in range(PACK):
                    v = u_tiles[bt][pair][:, j, t, :]
                    zT = zT_tiles[bt, pair, j][:, t, :]
                    gain = gb_cols[:, t, g : g + 1]
                    bias = gb_cols[:, t, GROUPS + g : GROUPS + g + 1]
                    nc.vector.tensor_scalar(
                        out=v, in0=zT, scalar1=gain, scalar2=bias, op0=ALU.mult, op1=ALU.add
                    )

        def sigmoid(bt, pair, groups):
            if groups.start == 0:
                e_tiles[bt, pair] = e_pool.tile(
                    [P, 2, PACK, P], F32, align_bytes=64, tag="e", name="e%d_%d" % (bt, pair)
                )
            nc.scalar.activation(
                out=e_tiles[bt, pair][:, groups, :, :],
                in_=u_tiles[bt][pair][:, groups, :, :],
                func=ACT.Sigmoid,
                scale=-1.0,
            )

        def logs(bt, pair, groups):
            e_sb = e_tiles[bt, pair][:, groups, :, :]
            nc.scalar.activation(out=e_sb, in_=e_sb, func=ACT.Ln, bias=ln_floor[:])

        def tanh(bt, pair, groups):
            e_sb = e_tiles[bt, pair][:, groups, :, :]
            nc.scalar.activation(out=e_sb, in_=e_sb, func=ACT.Tanh, scale=-1.0)

        def multiply(bt, pair, groups):
            if (bt, pair) not in h_tiles:
                h_tiles[bt, pair] = h_pool.tile(
                    [P, 2, P, PACK], BF16, align_bytes=64, name="h%d_%d" % (bt, pair), tag="h"
                )
            for j in range(groups.start, groups.stop):
                h = h_tiles[bt, pair][:, j, :, :].rearrange("p (c i) t -> p c t i", i=4)
                v = u_tiles[bt][pair][:, j, :, :].rearrange("p t (c i) -> p c t i", i=4)
                e = e_tiles[bt, pair][:, j, :, :].rearrange("p t (c i) -> p c t i", i=4)
                engine = nc.gpsimd if bt == 0 and pair < GPSIMD_PAIRS else nc.vector
                engine.tensor_tensor(out=h, in0=v, in1=e, op=ALU.mult)

        acc = {}

        codes = {}

        def second_product(bt, pair, groups):
            opens = (bt, 0) not in acc
            if opens:
                for nt in range(NT):
                    acc[bt, nt] = (
                        psum_big.tile([P, N_TILE], F32, tag="big", name="acc0_%d" % nt)
                        if bt == 0
                        else psum_tp.tile([P, N_TILE], F32, tag="tp", name="acc1_%d" % nt)
                    )
            if (bt, pair) not in codes:
                codes[bt, pair] = (
                    h_pool.tile([P, 2, P], U32, align_bytes=64, name="hc%d_%d" % (bt, pair), tag="hc"),
                    h_pool.tile([P, 2, P], U8, align_bytes=64, name="hs%d_%d" % (bt, pair), tag="hs"),
                )
            h_codes, h_scales = codes[bt, pair]
            nc.vector.quantize_mx(
                out=h_codes[:, groups, :].rearrange("p j b -> p (j b)").bitcast(FP8X4),
                scales=h_scales[:, groups, :].rearrange("p j b -> p (j b)"),
                in_=h_tiles[bt, pair][:, groups, :, :].rearrange("p j b t -> p (j b t)"),
            )
            js = range(groups.start, groups.stop)
            closes = pair == PAIRS - 1
            if not closes:
                order = [(j, nt) for j in js for nt in range(NT)]
            else:
                order = [(j, nt) for nt in range(NT) for j in js]
            for j, nt in order:
                g = 2 * pair + j
                a, k = divmod(g, PLANES)
                cols = slice(nt * N_TILE, (nt + 1) * N_TILE)
                nc.tensor.matmul_mx(
                    out=acc[bt, nt][:],
                    lhsT=h_codes[:, j, :].bitcast(FP8X4),
                    lhsT_scale=h_scales[:, j, :],
                    rhs=d3_tiles[g][:, cols].bitcast(FP8X4),
                    rhs_scale=d3_scales_sb[4 * k : P, a, cols],
                    start=opens and j == groups.start,
                    stop=closes and j == groups.stop - 1,
                )

        y_tiles = {}

        pieces = [
            [(nt, 0, N_TILE) for nt in range(NT)],
            [(nt, 0, N_TILE) for nt in range(NT - 1)]
            + [(NT - 1, 0, N_TILE // 2), (NT - 1, N_TILE // 2, N_TILE)],
        ]

        def add_bias(bt):
            for nt, first, last in pieces[bt]:
                if first == 0:
                    y_tiles[bt, nt] = e_pool.tile(
                        [P, N_TILE], F32, align_bytes=64, tag="e", name="y%d_%d" % (bt, nt)
                    )
                nc.vector.tensor_tensor(
                    out=y_tiles[bt, nt][:, first:last],
                    in0=acc[bt, nt][:, first:last],
                    in1=bo_bc[:, nt * N_TILE + first : nt * N_TILE + last],
                    op=ALU.add,
                )

        def store(bt):
            for nt, first, last in pieces[bt]:
                y = y_tiles[bt, nt][:, first:last]
                nc.scalar.activation(out=y, in_=y, func=ACT.Sigmoid)
                nc.sync.dma_start(
                    out=out[bt * P : (bt + 1) * P, nt * N_TILE + first : nt * N_TILE + last], in_=y
                )

        transpose(0, 0)
        for pair in range(PAIRS):
            if pair + 1 < PAIRS:
                transpose(0, pair + 1)
            for groups in HALVES if pair == 0 else [BOTH]:
                scale(0, pair, groups)
                sigmoid(0, pair, groups)
            if KEPT_EARLY + pair < KEPT:
                copy_out(1, KEPT_EARLY + pair)
        for pair in range(PAIRS):
            logs(0, pair, BOTH)
        for g in range(GROUPS):
            group_statistics(1, g, u_group(1, g) if g < KEPT else first_product(1, g)[:])
        load_d3(D3_EARLY, D3_EARLY + KEPT // D2_TILE_GROUPS)
        statistics(1)
        for g in range(KEPT):
            normalise(nc.gpsimd, 1, g)

        load_sigmoid_table()
        for pair in range(PAIRS):
            tanh(0, pair, BOTH)
        again = list(range(KEPT, GROUPS))
        for pair in range(4):
            for g in again[3 * pair : 3 * pair + 3]:
                multiply_and_normalise(1, g)
                if (g + 1) % D2_TILE_GROUPS == 0 or g + 1 == GROUPS:
                    load_d3(len(d3_tiles), len(d3_tiles) + 1)
            if pair == 0:
                transpose(1, 0)
            transpose(1, pair + 1)
            scale(1, pair, BOTH)
            sigmoid(1, pair, BOTH)

        bo_bc = const.tile([P, N_OUT], BF16)
        nc.sync.dma_start(out=bo_bc[:], in_=bo.partition_broadcast(P))

        transpose(1, 5)
        scale(1, 4, BOTH)
        sigmoid(1, 4, BOTH)
        for pair in range(5, PAIRS):
            if pair + 1 < PAIRS:
                transpose(1, pair + 1)
            scale(1, pair, BOTH)
            multiply(0, pair - 5, BOTH)
            sigmoid(1, pair, BOTH)
        for pair in range(3, PAIRS):
            second_product(0, pair - 3, BOTH)
            multiply(0, pair, BOTH)
        for pair in range(PAIRS - 3, PAIRS - 1):
            second_product(0, pair, BOTH)
        second_product(0, PAIRS - 1, BOTH)
        last = PAIRS - 1
        steps = [(0, HALVES[0]), (0, HALVES[1])] + [(pair, BOTH) for pair in range(1, last)]
        for pair in range(last):
            logs(1, pair, BOTH)
        load_sigmoid_table()
        for i, (pair, groups) in enumerate(steps):
            tanh(1, pair, groups)
            multiply(1, pair, groups)
            if i > 1:
                second_product(1, *steps[i - 1])
            if i == 0:
                second_product(1, pair, groups)
        second_product(1, *steps[-1])
        add_bias(0)
        logs(1, last, BOTH)
        load_sigmoid_table()
        for groups in HALVES:
            tanh(1, last, groups)
            multiply(1, last, groups)
        second_product(1, last, BOTH)
        store(0)
        add_bias(1)
        store(1)
